import numpy as np
import ml_dtypes


def mxq(x, axis, fmt="e4m3"):
    dtype, down = {"e4m3": (ml_dtypes.float8_e4m3fn, 7), "e5m2": (ml_dtypes.float8_e5m2, 14)}[fmt]
    v = np.moveaxis(np.asarray(x, np.float32).astype(ml_dtypes.bfloat16).astype(np.float64), axis, -1)
    blocks = v.reshape(v.shape[:-1] + (-1, 32))
    amax = np.abs(blocks).max(-1, keepdims=True)
    byte = np.maximum(np.where(amax > 0, np.frexp(amax)[1] - 1 + 127, 0) - down, 1)
    scale = np.exp2(byte - 127.0)
    codes = (blocks / scale).astype(np.float32).astype(dtype).astype(np.float64)
    return np.moveaxis((codes * scale).reshape(v.shape), -1, axis)


WIDE = False


def mx_kscale(k):
    if not WIDE:
        return np.ones(k)
    levels = np.array([10, -10, 5, -5, 0])
    a = np.random.permutation(np.resize(levels, k // 512 * 4)).reshape(k // 512, 4)
    idx = np.arange(k)
    return np.exp2(a[idx // 512, idx % 128 // 32])


BF16 = ml_dtypes.bfloat16


def bf(x):
    return np.asarray(x, np.float32).astype(BF16)


def f64(x):
    return np.asarray(x).astype(np.float64)


N, H, S, R, T = 16384, 512, 4, 128, 128


def setup_inputs():
    s = mx_kscale(H)
    return {"encodings": bf(np.random.standard_normal((N, H)) * s),
            "domain_encs": bf(np.random.standard_normal((S, H)) * s),
            "Us": bf(np.random.standard_normal((S, H, R)) / np.sqrt(H) / s[None, :, None])}


def reference(encodings, domain_encs, Us):
    diff = f64(encodings)[None, :, :] - f64(domain_encs)[:, None, :]
    proj = mxq(diff, 2, "e4m3") @ mxq(f64(Us), 1, "e4m3")
    dist = np.sqrt(np.sum(proj * proj, axis=-1))
    z = -dist
    e = np.exp(z - z.max(axis=0, keepdims=True))
    return e / e.sum(axis=0, keepdims=True)

@@ -1,0 +1,177 @@
+from contextlib import ExitStack
+
+import concourse.mybir as mybir
+from concourse.masks import make_identity
+
+F32 = mybir.dt.float32
+BF16 = mybir.dt.bfloat16
+U32 = mybir.dt.uint32
+U8 = mybir.dt.uint8
+FP8X4 = mybir.dt.float8_e4m3fn_x4
+ALU = mybir.AluOpType
+ACT = mybir.ActivationFunctionType
+AX = mybir.AxisListType
+
+P = 128
+N_TOK = 16384
+H = 512
+S = 4
+R = 128
+PACK = 4
+TILES = N_TOK // P
+TPB = 2
+COLS = TPB * P
+NB = TILES // TPB
+CHUNKS = (2, 2, 4, 8, 16, 16, 16, 16, 16, 16, 16)
+
+FLOPS = 2 * S * N_TOK * H * R
+
+
+def tile_moe_pa_t_kernel(tc, encodings, domain_encs, Us, out):
+    nc = tc.nc
+    with ExitStack() as ctx:
+        const = ctx.enter_context(tc.tile_pool(name="const", bufs=1))
+        encp = ctx.enter_context(tc.tile_pool(name="encp", bufs=1))
+        diffp = ctx.enter_context(tc.tile_pool(name="diffp", bufs=4))
+        codep = ctx.enter_context(tc.tile_pool(name="codep", bufs=3))
+        junkp = ctx.enter_context(tc.tile_pool(name="junkp", bufs=2))
+        xtp = ctx.enter_context(tc.psum_pool(name="xtp", bufs=3))
+        projp = ctx.enter_context(tc.psum_pool(name="projp", bufs=4))
+        ctx.enter_context(tc.manual_schedule())
+
+        raw_u = const.tile([P, S, PACK, R], BF16)
+        nc.scalar.dma_start(
+            out=raw_u[:].rearrange("p s (u e) r -> p (s u) (e r)", u=2),
+            in_=Us.rearrange("s (u p e) r -> p (s u) (e r)", u=2, p=P, e=2),
+        )
+        dom_t = const.tile([P, S, PACK], BF16)
+        nc.scalar.dma_start(
+            out=dom_t[:].rearrange("p s (u e) -> p (s u) e", u=2),
+            in_=domain_encs.rearrange("s (u p e) -> p (s u) e", u=2, p=P, e=2),
+        )
+        enc_view = encodings.rearrange("(p j) h -> p j h", j=TILES)
+        enc_of_tile = []
+        j0 = 0
+        for c, n in enumerate(CHUNKS):
+            enc_c = encp.tile([P, n, H], BF16, name="enc%d" % c)
+            nc.sync.dma_start(out=enc_c[:], in_=enc_view[:, j0 : j0 + n, :])
+            for jj in range(n):
+                enc_of_tile.append((enc_c, jj))
+            j0 += n
+
+        ident = const.tile([P, P], F32)
+        make_identity(nc, ident[:])
+
+        one = const.tile([P, 1], F32)
+        nc.vector.memset(one[:], 1.0)
+        warm = const.tile([P, 1], F32)
+        nc.scalar.activation(out=warm[:], in_=one[:], func=ACT.Sqrt)
+
+        grouped_u = const.tile([P, S, R, PACK], BF16, align_bytes=64)
+        nc.vector.tensor_copy(out=grouped_u[:], in_=raw_u[:].rearrange("p s t r -> p s r t"))
+        u_codes = const.tile([P, S * R], U32, align_bytes=64)
+        u_scales = const.tile([P, S * R], U8, align_bytes=64)
+
+        d2 = const.tile([P, TILES * S], F32)
+
+        xt_of = {}
+        diff_of = {}
+        code_of = {}
+
+        def transposes(b):
+            xt = xtp.tile([P, COLS, 2], F32, name="xt")
+            xt_of[b] = xt
+            for j2 in range(TPB):
+                enc_c, jj = enc_of_tile[b * TPB + j2]
+                words = enc_c[:, jj, :].bitcast(F32)
+                for u in range(2):
+                    nc.tensor.transpose(
+                        xt[:, j2 * P : (j2 + 1) * P, u], words[:, u * P : (u + 1) * P], ident[:]
+                    )
+
+        def subtract(b):
+            diff = diffp.tile([P, S, COLS, PACK], BF16, name="diff", align_bytes=64)
+            diff_of[b] = diff
+            nc.vector.tensor_tensor(
+                out=diff[:],
+                in0=xt_of[b][:].bitcast(BF16).unsqueeze(1).to_broadcast([P, S, COLS, PACK]),
+                in1=dom_t[:].unsqueeze(2).to_broadcast([P, S, COLS, PACK]),
+                op=ALU.subtract,
+            )
+
+        def quantise(b):
+            codes = codep.tile([P, S * COLS], U32, name="codes", align_bytes=64)
+            scales = codep.tile([P, S * COLS], U8, name="scales", align_bytes=64)
+            code_of[b] = (codes, scales)
+            nc.vector.quantize_mx(
+                out=codes[:].bitcast(FP8X4),
+                scales=scales[:],
+                in_=diff_of[b][:].rearrange("p s c t -> p (s c t)"),
+            )
+
+        def project(b):
+            codes, scales = code_of[b]
+            junk = junkp.tile([P, TPB * S, R], BF16, name="junk")
+            for j2 in range(TPB):
+                proj = projp.tile([P, S * R], F32, name="proj")
+                for s in range(S):
+                    tok = slice(s * COLS + j2 * P, s * COLS + (j2 + 1) * P)
+                    rr = slice(s * R, (s + 1) * R)
+                    nc.tensor.matmul_mx(
+                        out=proj[:, rr],
+                        lhsT=codes[:, tok].bitcast(FP8X4),
+                        lhsT_scale=scales[:, tok],
+                        rhs=u_codes[:, rr].bitcast(FP8X4),
+                        rhs_scale=u_scales[:, rr],
+                        start=True,
+                        stop=True,
+                    )
+                for s in range(S):
+                    col = (b * TPB + j2) * S + s
+                    nc.scalar.activation(
+                        out=junk[:, j2 * S + s, :],
+                        in_=proj[:, s * R : (s + 1) * R],
+                        func=ACT.Square,
+                        accum_out=d2[:, col : col + 1],
+                    )
+
+        transposes(0)
+        transposes(1)
+        subtract(0)
+        nc.vector.quantize_mx(
+            out=u_codes[:].bitcast(FP8X4),
+            scales=u_scales[:],
+            in_=grouped_u[:].rearrange("p s r t -> p (s r t)"),
+        )
+        for i in range(NB + 1):
+            if i + 2 < NB:
+                transposes(i + 2)
+            if i + 1 < NB:
+                subtract(i + 1)
+            if i < NB:
+                quantise(i)
+            if i >= 1:
+                project(i - 1)
+
+        dist = const.tile([P, TILES, S], F32)
+        nc.scalar.activation(out=dist[:].rearrange("p j s -> p (j s)"), in_=d2[:], func=ACT.Sqrt)
+        low = const.tile([P, TILES], F32)
+        nc.vector.tensor_reduce(out=low[:], in_=dist[:], axis=AX.X, op=ALU.min)
+        above = const.tile([P, TILES, S], F32)
+        nc.vector.tensor_tensor(
+            out=above[:], in0=dist[:], in1=low[:].unsqueeze(2).to_broadcast([P, TILES, S]), op=ALU.subtract
+        )
+        ex = const.tile([P, TILES, S], F32)
+        nc.scalar.activation(out=ex[:], in_=above[:], func=ACT.Exp, scale=-1.0)
+        total = const.tile([P, TILES], F32)
+        nc.vector.tensor_reduce(out=total[:], in_=ex[:], axis=AX.X, op=ALU.add)
+        inv = const.tile([P, TILES], F32)
+        nc.vector.reciprocal(out=inv[:], in_=total[:])
+        res = const.tile([P, S, TILES], F32)
+        nc.vector.tensor_tensor(
+            out=res[:],
+            in0=ex[:].rearrange("p j s -> p s j"),
+            in1=inv[:].unsqueeze(1).to_broadcast([P, S, TILES]),
+            op=ALU.mult,
+        )
+        nc.sync.dma_start(out=out.rearrange("s (p j) -> p s j", j=TILES), in_=res[:])

@@ -22,6 +22,8 @@ TILES = N_TOK // P
 TPB = 2
 COLS = TPB * P
 NB = TILES // TPB
+GC = 44
+CV = COLS - GC
 CHUNKS = (2, 2, 4, 8, 16, 16, 16, 16, 16, 16, 16)
 
 FLOPS = 2 * S * N_TOK * H * R
@@ -32,10 +34,11 @@ def tile_moe_pa_t_kernel(tc, encodings, domain_encs, Us, out):
     with ExitStack() as ctx:
         const = ctx.enter_context(tc.tile_pool(name="const", bufs=1))
         encp = ctx.enter_context(tc.tile_pool(name="encp", bufs=1))
-        diffp = ctx.enter_context(tc.tile_pool(name="diffp", bufs=4))
+        diffp = ctx.enter_context(tc.tile_pool(name="diffp", bufs=3))
+        xsp = ctx.enter_context(tc.tile_pool(name="xsp", bufs=4))
         codep = ctx.enter_context(tc.tile_pool(name="codep", bufs=3))
         junkp = ctx.enter_context(tc.tile_pool(name="junkp", bufs=2))
-        xtp = ctx.enter_context(tc.psum_pool(name="xtp", bufs=3))
+        xtp = ctx.enter_context(tc.psum_pool(name="xtp", bufs=4))
         projp = ctx.enter_context(tc.psum_pool(name="projp", bufs=4))
         ctx.enter_context(tc.manual_schedule())
 
@@ -75,6 +78,7 @@ def tile_moe_pa_t_kernel(tc, encodings, domain_encs, Us, out):
         d2 = const.tile([P, TILES * S], F32)
 
         xt_of = {}
+        xs_of = {}
         diff_of = {}
         code_of = {}
 
@@ -89,13 +93,26 @@ def tile_moe_pa_t_kernel(tc, encodings, domain_encs, Us, out):
                         xt[:, j2 * P : (j2 + 1) * P, u], words[:, u * P : (u + 1) * P], ident[:]
                     )
 
-        def subtract(b):
+        def side_copy(b):
+            xs = xsp.tile([P, GC, 2], F32, name="xs")
+            xs_of[b] = xs
+            nc.scalar.copy(out=xs[:], in_=xt_of[b][:, CV:COLS, :])
+
+        def side_subtract(b):
             diff = diffp.tile([P, S, COLS, PACK], BF16, name="diff", align_bytes=64)
             diff_of[b] = diff
+            nc.gpsimd.tensor_tensor(
+                out=diff[:, :, CV:COLS, :],
+                in0=xs_of[b][:].bitcast(BF16).unsqueeze(1).to_broadcast([P, S, GC, PACK]),
+                in1=dom_t[:].unsqueeze(2).to_broadcast([P, S, GC, PACK]),
+                op=ALU.subtract,
+            )
+
+        def subtract(b):
             nc.vector.tensor_tensor(
-                out=diff[:],
-                in0=xt_of[b][:].bitcast(BF16).unsqueeze(1).to_broadcast([P, S, COLS, PACK]),
-                in1=dom_t[:].unsqueeze(2).to_broadcast([P, S, COLS, PACK]),
+                out=diff_of[b][:, :, 0:CV, :],
+                in0=xt_of[b][:, 0:CV, :].bitcast(BF16).unsqueeze(1).to_broadcast([P, S, CV, PACK]),
+                in1=dom_t[:].unsqueeze(2).to_broadcast([P, S, CV, PACK]),
                 op=ALU.subtract,
             )
 
@@ -135,8 +152,10 @@ def tile_moe_pa_t_kernel(tc, encodings, domain_encs, Us, out):
                         accum_out=d2[:, col : col + 1],
                     )
 
-        transposes(0)
-        transposes(1)
+        for b in range(3):
+            transposes(b)
+            side_copy(b)
+            side_subtract(b)
         subtract(0)
         nc.vector.quantize_mx(
             out=u_codes[:].bitcast(FP8X4),
@@ -144,12 +163,15 @@ def tile_moe_pa_t_kernel(tc, encodings, domain_encs, Us, out):
             in_=grouped_u[:].rearrange("p s r t -> p (s r t)"),
         )
         for i in range(NB + 1):
-            if i + 2 < NB:
-                transposes(i + 2)
+            if i + 3 < NB:
+                transposes(i + 3)
+                side_copy(i + 3)
             if i + 1 < NB:
                 subtract(i + 1)
             if i < NB:
                 quantise(i)
+            if i + 3 < NB:
+                side_subtract(i + 3)
             if i >= 1:
                 project(i - 1)
 

@@ -22,11 +22,21 @@ TILES = N_TOK // P
 TPB = 2
 COLS = TPB * P
 NB = TILES // TPB
-GC = 44
+GC = 36
 CV = COLS - GC
-CHUNKS = (2, 2, 4, 8, 16, 16, 16, 16, 16, 16, 16)
+NS = 12
+NV = NB - NS
+JOBS = NS * TPB * S
+T0 = 4
+T1 = NV - 4
+SMALL_CHUNKS = (2, 2, 4, 8)
+BIG = 16
 
 FLOPS = 2 * S * N_TOK * H * R
+
+
+def job_tick(n):
+    return T0 + (n * (T1 - T0)) // JOBS
 
 
 def tile_moe_pa_t_kernel(tc, encodings, domain_encs, Us, out):
@@ -34,17 +44,21 @@ def tile_moe_pa_t_kernel(tc, encodings, domain_encs, Us, out):
     with ExitStack() as ctx:
         const = ctx.enter_context(tc.tile_pool(name="const", bufs=1))
         encp = ctx.enter_context(tc.tile_pool(name="encp", bufs=1))
+        bigp = ctx.enter_context(tc.tile_pool(name="bigp", bufs=3))
         diffp = ctx.enter_context(tc.tile_pool(name="diffp", bufs=3))
+        diffsp = ctx.enter_context(tc.tile_pool(name="diffsp", bufs=2))
         xsp = ctx.enter_context(tc.tile_pool(name="xsp", bufs=4))
-        codep = ctx.enter_context(tc.tile_pool(name="codep", bufs=3))
+        xfp = ctx.enter_context(tc.tile_pool(name="xfp", bufs=2))
+        codep = ctx.enter_context(tc.tile_pool(name="codep", bufs=4))
         junkp = ctx.enter_context(tc.tile_pool(name="junkp", bufs=2))
-        xtp = ctx.enter_context(tc.psum_pool(name="xtp", bufs=4))
-        projp = ctx.enter_context(tc.psum_pool(name="projp", bufs=4))
+        xtp = ctx.enter_context(tc.psum_pool(name="xtp", bufs=3))
+        projp = ctx.enter_context(tc.psum_pool(name="projp", bufs=2))
+        accp = ctx.enter_context(tc.psum_pool(name="accp", bufs=3))
         ctx.enter_context(tc.manual_schedule())
 
-        raw_u = const.tile([P, S, PACK, R], BF16)
+        raw_a = const.tile([P, S, PACK, R], BF16)
         nc.scalar.dma_start(
-            out=raw_u[:].rearrange("p s (u e) r -> p (s u) (e r)", u=2),
+            out=raw_a[:].rearrange("p s (u e) r -> p (s u) (e r)", u=2),
             in_=Us.rearrange("s (u p e) r -> p (s u) (e r)", u=2, p=P, e=2),
         )
         dom_t = const.tile([P, S, PACK], BF16)
@@ -52,15 +66,45 @@ def tile_moe_pa_t_kernel(tc, encodings, domain_encs, Us, out):
             out=dom_t[:].rearrange("p s (u e) -> p (s u) e", u=2),
             in_=domain_encs.rearrange("s (u p e) -> p (s u) e", u=2, p=P, e=2),
         )
+        raw_b = const.tile([P, S, PACK, R], BF16)
+        nc.scalar.dma_start(
+            out=raw_b[:].rearrange("p s t r -> p (s t) r"),
+            in_=Us.rearrange("s (t p) r -> p (s t) r", p=P),
+        )
+
         enc_view = encodings.rearrange("(p j) h -> p j h", j=TILES)
         enc_of_tile = []
-        j0 = 0
-        for c, n in enumerate(CHUNKS):
-            enc_c = encp.tile([P, n, H], BF16, name="enc%d" % c)
+        chunk_starts = []
+
+        def load_chunk():
+            j0 = len(enc_of_tile)
+            c = len(chunk_starts)
+            chunk_starts.append(j0)
+            if c < len(SMALL_CHUNKS):
+                n = SMALL_CHUNKS[c]
+                enc_c = encp.tile([P, n, H], BF16, name="enc%d" % c)
+            else:
+                n = BIG
+                enc_c = bigp.tile([P, n, H], BF16, name="encbig")
             nc.sync.dma_start(out=enc_c[:], in_=enc_view[:, j0 : j0 + n, :])
             for jj in range(n):
                 enc_of_tile.append((enc_c, jj))
-            j0 += n
+
+        for c in range(len(SMALL_CHUNKS)):
+            load_chunk()
+        dom_rep = const.tile([P, S * H], BF16)
+        nc.sync.dma_start(out=dom_rep[:], in_=domain_encs.rearrange("s h -> (s h)").partition_broadcast(P))
+        load_chunk()
+        load_chunk()
+
+        banks = []
+
+        def take_bank():
+            b = len(banks)
+            banks.append(b)
+            if b * TPB in chunk_starts[len(SMALL_CHUNKS) :] and len(enc_of_tile) < TILES:
+                load_chunk()
+            return b
 
         ident = const.tile([P, P], F32)
         make_identity(nc, ident[:])
@@ -70,21 +114,29 @@ def tile_moe_pa_t_kernel(tc, encodings, domain_encs, Us, out):
         warm = const.tile([P, 1], F32)
         nc.scalar.activation(out=warm[:], in_=one[:], func=ACT.Sqrt)
 
-        grouped_u = const.tile([P, S, R, PACK], BF16, align_bytes=64)
-        nc.vector.tensor_copy(out=grouped_u[:], in_=raw_u[:].rearrange("p s t r -> p s r t"))
-        u_codes = const.tile([P, S * R], U32, align_bytes=64)
-        u_scales = const.tile([P, S * R], U8, align_bytes=64)
+        grouped_a = const.tile([P, S, R, PACK], BF16, align_bytes=64)
+        grouped_b = const.tile([P, S, R, PACK], BF16, align_bytes=64)
+        ua_codes = const.tile([P, S * R], U32, align_bytes=64)
+        ua_scales = const.tile([P, S * R], U8, align_bytes=64)
+        ub_codes = const.tile([P, S * R], U32, align_bytes=64)
+        ub_scales = const.tile([P, S * R], U8, align_bytes=64)
+        neg_dom = const.tile([P, S, H], F32)
 
         d2 = const.tile([P, TILES * S], F32)
 
+        bank_of = {}
         xt_of = {}
         xs_of = {}
         diff_of = {}
         code_of = {}
+        xf_of = {}
+        acc_of = {}
 
-        def transposes(b):
+        def transposes(v):
+            b = take_bank()
+            bank_of[("v", v)] = b
             xt = xtp.tile([P, COLS, 2], F32, name="xt")
-            xt_of[b] = xt
+            xt_of[v] = xt
             for j2 in range(TPB):
                 enc_c, jj = enc_of_tile[b * TPB + j2]
                 words = enc_c[:, jj, :].bitcast(F32)
@@ -93,41 +145,76 @@ def tile_moe_pa_t_kernel(tc, encodings, domain_encs, Us, out):
                         xt[:, j2 * P : (j2 + 1) * P, u], words[:, u * P : (u + 1) * P], ident[:]
                     )
 
-        def side_copy(b):
+        def side_copy(v):
             xs = xsp.tile([P, GC, 2], F32, name="xs")
-            xs_of[b] = xs
-            nc.scalar.copy(out=xs[:], in_=xt_of[b][:, CV:COLS, :])
+            xs_of[v] = xs
+            nc.scalar.copy(out=xs[:], in_=xt_of[v][:, CV:COLS, :])
 
-        def side_subtract(b):
+        def side_subtract(v):
             diff = diffp.tile([P, S, COLS, PACK], BF16, name="diff", align_bytes=64)
-            diff_of[b] = diff
+            diff_of[("v", v)] = diff
             nc.gpsimd.tensor_tensor(
                 out=diff[:, :, CV:COLS, :],
-                in0=xs_of[b][:].bitcast(BF16).unsqueeze(1).to_broadcast([P, S, GC, PACK]),
+                in0=xs_of[v][:].bitcast(BF16).unsqueeze(1).to_broadcast([P, S, GC, PACK]),
                 in1=dom_t[:].unsqueeze(2).to_broadcast([P, S, GC, PACK]),
                 op=ALU.subtract,
             )
 
-        def subtract(b):
+        def subtract(v):
             nc.vector.tensor_tensor(
-                out=diff_of[b][:, :, 0:CV, :],
-                in0=xt_of[b][:, 0:CV, :].bitcast(BF16).unsqueeze(1).to_broadcast([P, S, CV, PACK]),
+                out=diff_of[("v", v)][:, :, 0:CV, :],
+                in0=xt_of[v][:, 0:CV, :].bitcast(BF16).unsqueeze(1).to_broadcast([P, S, CV, PACK]),
                 in1=dom_t[:].unsqueeze(2).to_broadcast([P, S, CV, PACK]),
                 op=ALU.subtract,
             )
 
-        def quantise(b):
+        def widen(q):
+            b = take_bank()
+            bank_of[("s", q)] = b
+            enc_c, jj = enc_of_tile[b * TPB]
+            xf = xfp.tile([P, TPB, H], F32, name="xf")
+            xf_of[q] = xf
+            nc.scalar.copy(out=xf[:], in_=enc_c[:, jj : jj + TPB, :])
+
+        def tensor_subtract(n):
+            q, k = divmod(n, TPB * S)
+            j2, s = divmod(k, S)
+            acc = accp.tile([P, PACK, P], F32, name="acc")
+            acc_of[n] = acc
+            for t in range(PACK):
+                ks = slice(t * P, (t + 1) * P)
+                nc.tensor.matmul(
+                    out=acc[:, t, :], lhsT=xf_of[q][:, j2, ks], rhs=ident[:], is_transpose=True, start=True, stop=False
+                )
+                nc.tensor.matmul(
+                    out=acc[:, t, :], lhsT=neg_dom[:, s, ks], rhs=ident[:], is_transpose=True, start=False, stop=True
+                )
+
+        def round_out(n):
+            q, k = divmod(n, TPB * S)
+            j2, s = divmod(k, S)
+            if k == 0:
+                diff_s = diffsp.tile([P, S, COLS, PACK], BF16, name="diff_s", align_bytes=64)
+                diff_of[("s", q)] = diff_s
+            nc.scalar.copy(
+                out=diff_of[("s", q)][:, s, j2 * P : (j2 + 1) * P, :],
+                in_=acc_of[n][:].rearrange("p t c -> p c t"),
+            )
+
+        def quantise(key):
             codes = codep.tile([P, S * COLS], U32, name="codes", align_bytes=64)
             scales = codep.tile([P, S * COLS], U8, name="scales", align_bytes=64)
-            code_of[b] = (codes, scales)
+            code_of[key] = (codes, scales)
             nc.vector.quantize_mx(
                 out=codes[:].bitcast(FP8X4),
                 scales=scales[:],
-                in_=diff_of[b][:].rearrange("p s c t -> p (s c t)"),
+                in_=diff_of[key][:].rearrange("p s c t -> p (s c t)"),
             )
 
-        def project(b):
-            codes, scales = code_of[b]
+        def project(key):
+            codes, scales = code_of[key]
+            b = bank_of[key]
+            u_codes, u_scales = (ua_codes, ua_scales) if key[0] == "v" else (ub_codes, ub_scales)
             junk = junkp.tile([P, TPB * S, R], BF16, name="junk")
             for j2 in range(TPB):
                 proj = projp.tile([P, S * R], F32, name="proj")
@@ -152,28 +239,55 @@ def tile_moe_pa_t_kernel(tc, encodings, domain_encs, Us, out):
                         accum_out=d2[:, col : col + 1],
                     )
 
-        for b in range(3):
-            transposes(b)
-            side_copy(b)
-            side_subtract(b)
+        jobs_at = {}
+        for n in range(JOBS):
+            jobs_at[job_tick(n)] = jobs_at.get(job_tick(n), []) + [n]
+        widen_at = dict((job_tick(q * TPB * S) - 1, q) for q in range(NS))
+        quant_at = dict((job_tick(q * TPB * S + TPB * S - 1) + 2, q) for q in range(NS))
+
+        nc.scalar.copy(out=grouped_a[:], in_=raw_a[:].rearrange("p s t r -> p s r t"))
+        for v in range(3):
+            transposes(v)
+            side_copy(v)
+            side_subtract(v)
+        nc.scalar.copy(out=grouped_b[:], in_=raw_b[:].rearrange("p s t r -> p s r t"))
         subtract(0)
         nc.vector.quantize_mx(
-            out=u_codes[:].bitcast(FP8X4),
-            scales=u_scales[:],
-            in_=grouped_u[:].rearrange("p s r t -> p (s r t)"),
+            out=ua_codes[:].bitcast(FP8X4),
+            scales=ua_scales[:],
+            in_=grouped_a[:].rearrange("p s r t -> p (s r t)"),
         )
-        for i in range(NB + 1):
-            if i + 3 < NB:
+
+        for i in range(NV + 1):
+            if i + 3 < NV:
                 transposes(i + 3)
                 side_copy(i + 3)
-            if i + 1 < NB:
+            if i == 2:
+                nc.scalar.mul(out=neg_dom[:].rearrange("p s h -> p (s h)"), in_=dom_rep[:], mul=-1.0)
+            for n in jobs_at.get(i - 1, []):
+                round_out(n)
+            for n in jobs_at.get(i, []):
+                tensor_subtract(n)
+            if i in widen_at:
+                widen(widen_at[i])
+            if i + 1 < NV:
                 subtract(i + 1)
-            if i < NB:
-                quantise(i)
-            if i + 3 < NB:
+            if i == 2:
+                nc.vector.quantize_mx(
+                    out=ub_codes[:].bitcast(FP8X4),
+                    scales=ub_scales[:],
+                    in_=grouped_b[:].rearrange("p s r t -> p (s r t)"),
+                )
+            if i in quant_at:
+                quantise(("s", quant_at[i]))
+            if i < NV:
+                quantise(("v", i))
+            if i + 3 < NV:
                 side_subtract(i + 3)
             if i >= 1:
-                project(i - 1)
+                project(("v", i - 1))
+            if i - 1 in quant_at:
+                project(("s", quant_at[i - 1]))
 
         dist = const.tile([P, TILES, S], F32)
         nc.scalar.activation(out=dist[:].rearrange("p j s -> p (j s)"), in_=d2[:], func=ACT.Sqrt)

@@ -24,11 +24,13 @@ COLS = TPB * P
 NB = TILES // TPB
 GC = 36
 CV = COLS - GC
-NS = 12
+NS = 10
 NV = NB - NS
 JOBS = NS * TPB * S
 T0 = 4
 T1 = NV - 4
+HEAD = 2
+PROJ_BUFS = 3
 SMALL_CHUNKS = (2, 2, 4, 8)
 BIG = 16
 
@@ -50,10 +52,10 @@ def tile_moe_pa_t_kernel(tc, encodings, domain_encs, Us, out):
         xsp = ctx.enter_context(tc.tile_pool(name="xsp", bufs=4))
         xfp = ctx.enter_context(tc.tile_pool(name="xfp", bufs=2))
         codep = ctx.enter_context(tc.tile_pool(name="codep", bufs=4))
-        junkp = ctx.enter_context(tc.tile_pool(name="junkp", bufs=2))
+        junkp = ctx.enter_context(tc.tile_pool(name="junkp", bufs=3))
         xtp = ctx.enter_context(tc.psum_pool(name="xtp", bufs=3))
-        projp = ctx.enter_context(tc.psum_pool(name="projp", bufs=2))
-        accp = ctx.enter_context(tc.psum_pool(name="accp", bufs=3))
+        projp = ctx.enter_context(tc.psum_pool(name="projp", bufs=PROJ_BUFS))
+        accp = ctx.enter_context(tc.psum_pool(name="accp", bufs=2))
         ctx.enter_context(tc.manual_schedule())
 
         raw_a = const.tile([P, S, PACK, R], BF16)
@@ -146,6 +148,8 @@ def tile_moe_pa_t_kernel(tc, encodings, domain_encs, Us, out):
                     )
 
         def side_copy(v):
+            if v < HEAD:
+                return
             xs = xsp.tile([P, GC, 2], F32, name="xs")
             xs_of[v] = xs
             nc.scalar.copy(out=xs[:], in_=xt_of[v][:, CV:COLS, :])
@@ -153,6 +157,8 @@ def tile_moe_pa_t_kernel(tc, encodings, domain_encs, Us, out):
         def side_subtract(v):
             diff = diffp.tile([P, S, COLS, PACK], BF16, name="diff", align_bytes=64)
             diff_of[("v", v)] = diff
+            if v < HEAD:
+                return
             nc.gpsimd.tensor_tensor(
                 out=diff[:, :, CV:COLS, :],
                 in0=xs_of[v][:].bitcast(BF16).unsqueeze(1).to_broadcast([P, S, GC, PACK]),
@@ -161,10 +167,11 @@ def tile_moe_pa_t_kernel(tc, encodings, domain_encs, Us, out):
             )
 
         def subtract(v):
+            cv = COLS if v < HEAD else CV
             nc.vector.tensor_tensor(
-                out=diff_of[("v", v)][:, :, 0:CV, :],
-                in0=xt_of[v][:, 0:CV, :].bitcast(BF16).unsqueeze(1).to_broadcast([P, S, CV, PACK]),
-                in1=dom_t[:].unsqueeze(2).to_broadcast([P, S, CV, PACK]),
+                out=diff_of[("v", v)][:, :, 0:cv, :],
+                in0=xt_of[v][:, 0:cv, :].bitcast(BF16).unsqueeze(1).to_broadcast([P, S, cv, PACK]),
+                in1=dom_t[:].unsqueeze(2).to_broadcast([P, S, cv, PACK]),
                 op=ALU.subtract,
             )
 
@@ -211,12 +218,28 @@ def tile_moe_pa_t_kernel(tc, encodings, domain_encs, Us, out):
                 in_=diff_of[key][:].rearrange("p s c t -> p (s c t)"),
             )
 
+        waiting = []
+        squared = []
+
+        def squares():
+            proj, tile_j = waiting[len(squared)]
+            squared.append(tile_j)
+            junk = junkp.tile([P, S, R], BF16, name="junk")
+            for s in range(S):
+                col = tile_j * S + s
+                nc.scalar.activation(
+                    out=junk[:, s, :],
+                    in_=proj[:, s * R : (s + 1) * R],
+                    func=ACT.Square,
+                    accum_out=d2[:, col : col + 1],
+                )
+
         def project(key):
             codes, scales = code_of[key]
-            b = bank_of[key]
             u_codes, u_scales = (ua_codes, ua_scales) if key[0] == "v" else (ub_codes, ub_scales)
-            junk = junkp.tile([P, TPB * S, R], BF16, name="junk")
             for j2 in range(TPB):
+                while len(waiting) - len(squared) >= PROJ_BUFS:
+                    squares()
                 proj = projp.tile([P, S * R], F32, name="proj")
                 for s in range(S):
                     tok = slice(s * COLS + j2 * P, s * COLS + (j2 + 1) * P)
@@ -230,14 +253,7 @@ def tile_moe_pa_t_kernel(tc, encodings, domain_encs, Us, out):
                         start=True,
                         stop=True,
                     )
-                for s in range(S):
-                    col = (b * TPB + j2) * S + s
-                    nc.scalar.activation(
-                        out=junk[:, j2 * S + s, :],
-                        in_=proj[:, s * R : (s + 1) * R],
-                        func=ACT.Square,
-                        accum_out=d2[:, col : col + 1],
-                    )
+                waiting.append((proj, bank_of[key] * TPB + j2))
 
         jobs_at = {}
         for n in range(JOBS):
@@ -245,33 +261,39 @@ def tile_moe_pa_t_kernel(tc, encodings, domain_encs, Us, out):
         widen_at = dict((job_tick(q * TPB * S) - 1, q) for q in range(NS))
         quant_at = dict((job_tick(q * TPB * S + TPB * S - 1) + 2, q) for q in range(NS))
 
-        nc.scalar.copy(out=grouped_a[:], in_=raw_a[:].rearrange("p s t r -> p s r t"))
         for v in range(3):
             transposes(v)
             side_copy(v)
             side_subtract(v)
+        nc.scalar.copy(out=grouped_a[:], in_=raw_a[:].rearrange("p s t r -> p s r t"))
         nc.scalar.copy(out=grouped_b[:], in_=raw_b[:].rearrange("p s t r -> p s r t"))
         subtract(0)
-        nc.vector.quantize_mx(
-            out=ua_codes[:].bitcast(FP8X4),
-            scales=ua_scales[:],
-            in_=grouped_a[:].rearrange("p s r t -> p (s r t)"),
-        )
 
         for i in range(NV + 1):
             if i + 3 < NV:
                 transposes(i + 3)
-                side_copy(i + 3)
+            if i >= 1:
+                project(("v", i - 1))
+            if i - 1 in quant_at:
+                project(("s", quant_at[i - 1]))
             if i == 2:
                 nc.scalar.mul(out=neg_dom[:].rearrange("p s h -> p (s h)"), in_=dom_rep[:], mul=-1.0)
             for n in jobs_at.get(i - 1, []):
                 round_out(n)
             for n in jobs_at.get(i, []):
                 tensor_subtract(n)
+            if i + 3 < NV:
+                side_copy(i + 3)
             if i in widen_at:
                 widen(widen_at[i])
             if i + 1 < NV:
                 subtract(i + 1)
+            if i == 0:
+                nc.vector.quantize_mx(
+                    out=ua_codes[:].bitcast(FP8X4),
+                    scales=ua_scales[:],
+                    in_=grouped_a[:].rearrange("p s r t -> p (s r t)"),
+                )
             if i == 2:
                 nc.vector.quantize_mx(
                     out=ub_codes[:].bitcast(FP8X4),
@@ -284,10 +306,8 @@ def tile_moe_pa_t_kernel(tc, encodings, domain_encs, Us, out):
                 quantise(("v", i))
             if i + 3 < NV:
                 side_subtract(i + 3)
-            if i >= 1:
-                project(("v", i - 1))
-            if i - 1 in quant_at:
-                project(("s", quant_at[i - 1]))
+        while len(squared) < len(waiting):
+            squares()
 
         dist = const.tile([P, TILES, S], F32)
         nc.scalar.activation(out=dist[:].rearrange("p j s -> p (j s)"), in_=d2[:], func=ACT.Sqrt)

@@ -19,6 +19,10 @@ S = 4
 R = 128
 PACK = 4
 TILES = N_TOK // P
+HALF = H // 2
+WORDS = HALF // 2
+CT = P // 2
+BPT = P // CT
 TPB = 2
 COLS = TPB * P
 NB = TILES // TPB
@@ -68,13 +72,8 @@ def tile_moe_pa_t_kernel(tc, encodings, domain_encs, Us, out):
             out=dom_t[:].rearrange("p s (u e) -> p (s u) e", u=2),
             in_=domain_encs.rearrange("s (u p e) -> p (s u) e", u=2, p=P, e=2),
         )
-        raw_b = const.tile([P, S, PACK, R], BF16)
-        nc.scalar.dma_start(
-            out=raw_b[:].rearrange("p s t r -> p (s t) r"),
-            in_=Us.rearrange("s (t p) r -> p (s t) r", p=P),
-        )
 
-        enc_view = encodings.rearrange("(p j) h -> p j h", j=TILES)
+        enc_view = encodings.rearrange("(j c) (u w) -> (c u) j w", c=CT, u=2)
         enc_of_tile = []
         chunk_starts = []
 
@@ -84,18 +83,21 @@ def tile_moe_pa_t_kernel(tc, encodings, domain_encs, Us, out):
             chunk_starts.append(j0)
             if c < len(SMALL_CHUNKS):
                 n = SMALL_CHUNKS[c]
-                enc_c = encp.tile([P, n, H], BF16, name="enc%d" % c)
+                enc_c = encp.tile([P, n * BPT, HALF], BF16, name="enc%d" % c)
             else:
                 n = BIG
-                enc_c = bigp.tile([P, n, H], BF16, name="encbig")
-            nc.sync.dma_start(out=enc_c[:], in_=enc_view[:, j0 : j0 + n, :])
+                enc_c = bigp.tile([P, n * BPT, HALF], BF16, name="encbig")
+            nc.sync.dma_start(out=enc_c[:], in_=enc_view[:, j0 * BPT : (j0 + n) * BPT, :])
             for jj in range(n):
                 enc_of_tile.append((enc_c, jj))
 
         for c in range(len(SMALL_CHUNKS)):
             load_chunk()
-        dom_rep = const.tile([P, S * H], BF16)
-        nc.sync.dma_start(out=dom_rep[:], in_=domain_encs.rearrange("s h -> (s h)").partition_broadcast(P))
+        dom_rep = const.tile([P, S, HALF], BF16)
+        for u in range(2):
+            nc.sync.dma_start(
+                out=dom_rep[u:P:2, :, :], in_=domain_encs[:, u * HALF : (u + 1) * HALF].partition_broadcast(CT)
+            )
         load_chunk()
         load_chunk()
 
@@ -117,14 +119,11 @@ def tile_moe_pa_t_kernel(tc, encodings, domain_encs, Us, out):
         nc.scalar.activation(out=warm[:], in_=one[:], func=ACT.Sqrt)
 
         grouped_a = const.tile([P, S, R, PACK], BF16, align_bytes=64)
-        grouped_b = const.tile([P, S, R, PACK], BF16, align_bytes=64)
         ua_codes = const.tile([P, S * R], U32, align_bytes=64)
         ua_scales = const.tile([P, S * R], U8, align_bytes=64)
-        ub_codes = const.tile([P, S * R], U32, align_bytes=64)
-        ub_scales = const.tile([P, S * R], U8, align_bytes=64)
-        neg_dom = const.tile([P, S, H], F32)
+        neg_dom = const.tile([P, S, 2, WORDS], F32)
 
-        d2 = const.tile([P, TILES * S], F32)
+        d2 = const.tile([P, S, TILES], F32)
 
         bank_of = {}
         xt_of = {}
@@ -141,10 +140,12 @@ def tile_moe_pa_t_kernel(tc, encodings, domain_encs, Us, out):
             xt_of[v] = xt
             for j2 in range(TPB):
                 enc_c, jj = enc_of_tile[b * TPB + j2]
-                words = enc_c[:, jj, :].bitcast(F32)
-                for u in range(2):
+                for i2 in range(BPT):
+                    c0 = j2 * P + i2 * CT
                     nc.tensor.transpose(
-                        xt[:, j2 * P : (j2 + 1) * P, u], words[:, u * P : (u + 1) * P], ident[:]
+                        xt[:, c0 : c0 + CT, :].rearrange("p c u -> p (c u)"),
+                        enc_c[:, jj * BPT + i2, :].bitcast(F32),
+                        ident[:],
                     )
 
         def side_copy(v):
@@ -179,23 +180,36 @@ def tile_moe_pa_t_kernel(tc, encodings, domain_encs, Us, out):
             b = take_bank()
             bank_of[("s", q)] = b
             enc_c, jj = enc_of_tile[b * TPB]
-            xf = xfp.tile([P, TPB, H], F32, name="xf")
+            xf = xfp.tile([P, TPB * BPT, 2, WORDS], F32, name="xf")
             xf_of[q] = xf
-            nc.scalar.copy(out=xf[:], in_=enc_c[:, jj : jj + TPB, :])
+            nc.scalar.copy(
+                out=xf[:],
+                in_=enc_c[:, jj * BPT : (jj + TPB) * BPT, :].rearrange("p j (w e) -> p j e w", e=2),
+            )
 
         def tensor_subtract(n):
             q, k = divmod(n, TPB * S)
             j2, s = divmod(k, S)
-            acc = accp.tile([P, PACK, P], F32, name="acc")
+            acc = accp.tile([P, BPT, 2, P], F32, name="acc")
             acc_of[n] = acc
-            for t in range(PACK):
-                ks = slice(t * P, (t + 1) * P)
-                nc.tensor.matmul(
-                    out=acc[:, t, :], lhsT=xf_of[q][:, j2, ks], rhs=ident[:], is_transpose=True, start=True, stop=False
-                )
-                nc.tensor.matmul(
-                    out=acc[:, t, :], lhsT=neg_dom[:, s, ks], rhs=ident[:], is_transpose=True, start=False, stop=True
-                )
+            for i2 in range(BPT):
+                for e in range(2):
+                    nc.tensor.matmul(
+                        out=acc[:, i2, e, :],
+                        lhsT=xf_of[q][:, j2 * BPT + i2, e, :],
+                        rhs=ident[:],
+                        is_transpose=True,
+                        start=True,
+                        stop=False,
+                    )
+                    nc.tensor.matmul(
+                        out=acc[:, i2, e, :],
+                        lhsT=neg_dom[:, s, e, :],
+                        rhs=ident[:],
+                        is_transpose=True,
+                        start=False,
+                        stop=True,
+                    )
 
         def round_out(n):
             q, k = divmod(n, TPB * S)
@@ -204,8 +218,10 @@ def tile_moe_pa_t_kernel(tc, encodings, domain_encs, Us, out):
                 diff_s = diffsp.tile([P, S, COLS, PACK], BF16, name="diff_s", align_bytes=64)
                 diff_of[("s", q)] = diff_s
             nc.scalar.copy(
-                out=diff_of[("s", q)][:, s, j2 * P : (j2 + 1) * P, :],
-                in_=acc_of[n][:].rearrange("p t c -> p c t"),
+                out=diff_of[("s", q)][:, s, j2 * P : (j2 + 1) * P, :]
+                .rearrange("p c t -> p (c t)")
+                .rearrange("p (i x e) -> p i x e", i=BPT, e=2),
+                in_=acc_of[n][:].rearrange("p i e c -> p i c e"),
             )
 
         def quantise(key):
@@ -226,17 +242,15 @@ def tile_moe_pa_t_kernel(tc, encodings, domain_encs, Us, out):
             squared.append(tile_j)
             junk = junkp.tile([P, S, R], BF16, name="junk")
             for s in range(S):
-                col = tile_j * S + s
                 nc.scalar.activation(
                     out=junk[:, s, :],
                     in_=proj[:, s * R : (s + 1) * R],
                     func=ACT.Square,
-                    accum_out=d2[:, col : col + 1],
+                    accum_out=d2[:, s, tile_j : tile_j + 1],
                 )
 
         def project(key):
             codes, scales = code_of[key]
-            u_codes, u_scales = (ua_codes, ua_scales) if key[0] == "v" else (ub_codes, ub_scales)
             for j2 in range(TPB):
                 while len(waiting) - len(squared) >= PROJ_BUFS:
                     squares()
@@ -248,8 +262,8 @@ def tile_moe_pa_t_kernel(tc, encodings, domain_encs, Us, out):
                         out=proj[:, rr],
                         lhsT=codes[:, tok].bitcast(FP8X4),
                         lhsT_scale=scales[:, tok],
-                        rhs=u_codes[:, rr].bitcast(FP8X4),
-                        rhs_scale=u_scales[:, rr],
+                        rhs=ua_codes[:, rr].bitcast(FP8X4),
+                        rhs_scale=ua_scales[:, rr],
                         start=True,
                         stop=True,
                     )
@@ -266,7 +280,6 @@ def tile_moe_pa_t_kernel(tc, encodings, domain_encs, Us, out):
             side_copy(v)
             side_subtract(v)
         nc.scalar.copy(out=grouped_a[:], in_=raw_a[:].rearrange("p s t r -> p s r t"))
-        nc.scalar.copy(out=grouped_b[:], in_=raw_b[:].rearrange("p s t r -> p s r t"))
         subtract(0)
 
         for i in range(NV + 1):
@@ -277,7 +290,7 @@ def tile_moe_pa_t_kernel(tc, encodings, domain_encs, Us, out):
             if i - 1 in quant_at:
                 project(("s", quant_at[i - 1]))
             if i == 2:
-                nc.scalar.mul(out=neg_dom[:].rearrange("p s h -> p (s h)"), in_=dom_rep[:], mul=-1.0)
+                nc.scalar.mul(out=neg_dom[:], in_=dom_rep[:].rearrange("p s (w e) -> p s e w", e=2), mul=-1.0)
             for n in jobs_at.get(i - 1, []):
                 round_out(n)
             for n in jobs_at.get(i, []):
@@ -294,12 +307,6 @@ def tile_moe_pa_t_kernel(tc, encodings, domain_encs, Us, out):
                     scales=ua_scales[:],
                     in_=grouped_a[:].rearrange("p s r t -> p (s r t)"),
                 )
-            if i == 2:
-                nc.vector.quantize_mx(
-                    out=ub_codes[:].bitcast(FP8X4),
-                    scales=ub_scales[:],
-                    in_=grouped_b[:].rearrange("p s r t -> p (s r t)"),
-                )
             if i in quant_at:
                 quantise(("s", quant_at[i]))
             if i < NV:
@@ -309,25 +316,25 @@ def tile_moe_pa_t_kernel(tc, encodings, domain_encs, Us, out):
         while len(squared) < len(waiting):
             squares()
 
-        dist = const.tile([P, TILES, S], F32)
-        nc.scalar.activation(out=dist[:].rearrange("p j s -> p (j s)"), in_=d2[:], func=ACT.Sqrt)
-        low = const.tile([P, TILES], F32)
-        nc.vector.tensor_reduce(out=low[:], in_=dist[:], axis=AX.X, op=ALU.min)
-        above = const.tile([P, TILES, S], F32)
+        d2t = projp.tile([P, S * R], F32, name="proj")
+        for s in range(S):
+            nc.tensor.transpose(d2t[:, s * P : (s + 1) * P], d2[:, s, :], ident[:])
+        dist = const.tile([P, S, P], F32)
+        nc.scalar.activation(out=dist[:].rearrange("j s p -> j (s p)"), in_=d2t[:], func=ACT.Sqrt)
+        low = const.tile([P, P], F32)
+        nc.vector.tensor_reduce(out=low[:], in_=dist[:].rearrange("j s p -> j p s"), axis=AX.X, op=ALU.min)
+        above = const.tile([P, S, P], F32)
         nc.vector.tensor_tensor(
-            out=above[:], in0=dist[:], in1=low[:].unsqueeze(2).to_broadcast([P, TILES, S]), op=ALU.subtract
+            out=above[:], in0=dist[:], in1=low[:].unsqueeze(1).to_broadcast([P, S, P]), op=ALU.subtract
         )
-        ex = const.tile([P, TILES, S], F32)
+        ex = const.tile([P, S, P], F32)
         nc.scalar.activation(out=ex[:], in_=above[:], func=ACT.Exp, scale=-1.0)
-        total = const.tile([P, TILES], F32)
-        nc.vector.tensor_reduce(out=total[:], in_=ex[:], axis=AX.X, op=ALU.add)
-        inv = const.tile([P, TILES], F32)
+        total = const.tile([P, P], F32)
+        nc.vector.tensor_reduce(out=total[:], in_=ex[:].rearrange("j s p -> j p s"), axis=AX.X, op=ALU.add)
+        inv = const.tile([P, P], F32)
         nc.vector.reciprocal(out=inv[:], in_=total[:])
-        res = const.tile([P, S, TILES], F32)
+        res = const.tile([P, S, P], F32)
         nc.vector.tensor_tensor(
-            out=res[:],
-            in0=ex[:].rearrange("p j s -> p s j"),
-            in1=inv[:].unsqueeze(1).to_broadcast([P, S, TILES]),
-            op=ALU.mult,
+            out=res[:], in0=ex[:], in1=inv[:].unsqueeze(1).to_broadcast([P, S, P]), op=ALU.mult
         )
-        nc.sync.dma_start(out=out.rearrange("s (p j) -> p s j", j=TILES), in_=res[:])
+        nc.sync.dma_start(out=out.rearrange("s (j p) -> j s p", p=P), in_=res[:])

@@ -28,11 +28,11 @@ COLS = TPB * P
 NB = TILES // TPB
 GC = 36
 CV = COLS - GC
-NS = 10
+NS = 12
 NV = NB - NS
 JOBS = NS * TPB * S
-T0 = 4
-T1 = NV - 4
+T0 = 2
+T1 = NV - 2
 HEAD = 2
 PROJ_BUFS = 3
 SMALL_CHUNKS = (2, 2, 4, 8)
@@ -52,7 +52,7 @@ def tile_moe_pa_t_kernel(tc, encodings, domain_encs, Us, out):
         encp = ctx.enter_context(tc.tile_pool(name="encp", bufs=1))
         bigp = ctx.enter_context(tc.tile_pool(name="bigp", bufs=3))
         diffp = ctx.enter_context(tc.tile_pool(name="diffp", bufs=3))
-        diffsp = ctx.enter_context(tc.tile_pool(name="diffsp", bufs=2))
+        diffsp = ctx.enter_context(tc.tile_pool(name="diffsp", bufs=3))
         xsp = ctx.enter_context(tc.tile_pool(name="xsp", bufs=4))
         xfp = ctx.enter_context(tc.tile_pool(name="xfp", bufs=2))
         codep = ctx.enter_context(tc.tile_pool(name="codep", bufs=4))
@@ -273,7 +273,7 @@ def tile_moe_pa_t_kernel(tc, encodings, domain_encs, Us, out):
         for n in range(JOBS):
             jobs_at[job_tick(n)] = jobs_at.get(job_tick(n), []) + [n]
         widen_at = dict((job_tick(q * TPB * S) - 1, q) for q in range(NS))
-        quant_at = dict((job_tick(q * TPB * S + TPB * S - 1) + 2, q) for q in range(NS))
+        quant_at = dict((min(job_tick(q * TPB * S + TPB * S - 1) + 3, NV - 1), q) for q in range(NS))
 
         for v in range(3):
             transposes(v)
@@ -289,7 +289,7 @@ def tile_moe_pa_t_kernel(tc, encodings, domain_encs, Us, out):
                 project(("v", i - 1))
             if i - 1 in quant_at:
                 project(("s", quant_at[i - 1]))
-            if i == 2:
+            if i == 1:
                 nc.scalar.mul(out=neg_dom[:], in_=dom_rep[:].rearrange("p s (w e) -> p s e w", e=2), mul=-1.0)
             for n in jobs_at.get(i - 1, []):
                 round_out(n)

@@ -34,11 +34,16 @@ JOBS = NS * TPB * S
 T0 = 2
 T1 = NV - 2
 HEAD = 2
+NP = 6
 PROJ_BUFS = 3
 SMALL_CHUNKS = (2, 2, 4, 8)
 BIG = 16
 
 FLOPS = 2 * S * N_TOK * H * R
+
+
+def plain(q):
+    return (q * NP) // NS != ((q + 1) * NP) // NS
 
 
 def job_tick(n):
@@ -50,7 +55,7 @@ def tile_moe_pa_t_kernel(tc, encodings, domain_encs, Us, out):
     with ExitStack() as ctx:
         const = ctx.enter_context(tc.tile_pool(name="const", bufs=1))
         encp = ctx.enter_context(tc.tile_pool(name="encp", bufs=1))
-        bigp = ctx.enter_context(tc.tile_pool(name="bigp", bufs=3))
+        bigp = ctx.enter_context(tc.tile_pool(name="bigp", bufs=4))
         diffp = ctx.enter_context(tc.tile_pool(name="diffp", bufs=3))
         diffsp = ctx.enter_context(tc.tile_pool(name="diffsp", bufs=3))
         xsp = ctx.enter_context(tc.tile_pool(name="xsp", bufs=4))
@@ -62,15 +67,15 @@ def tile_moe_pa_t_kernel(tc, encodings, domain_encs, Us, out):
         accp = ctx.enter_context(tc.psum_pool(name="accp", bufs=2))
         ctx.enter_context(tc.manual_schedule())
 
-        raw_a = const.tile([P, S, PACK, R], BF16)
-        nc.scalar.dma_start(
-            out=raw_a[:].rearrange("p s (u e) r -> p (s u) (e r)", u=2),
-            in_=Us.rearrange("s (u p e) r -> p (s u) (e r)", u=2, p=P, e=2),
-        )
         dom_t = const.tile([P, S, PACK], BF16)
         nc.scalar.dma_start(
             out=dom_t[:].rearrange("p s (u e) -> p (s u) e", u=2),
             in_=domain_encs.rearrange("s (u p e) -> p (s u) e", u=2, p=P, e=2),
+        )
+        raw_a = const.tile([P, S, PACK, R], BF16)
+        nc.scalar.dma_start(
+            out=raw_a[:].rearrange("p s (u e) r -> p (s u) (e r)", u=2),
+            in_=Us.rearrange("s (u p e) r -> p (s u) (e r)", u=2, p=P, e=2),
         )
 
         enc_view = encodings.rearrange("(j c) (u w) -> (c u) j w", c=CT, u=2)
@@ -112,6 +117,8 @@ def tile_moe_pa_t_kernel(tc, encodings, domain_encs, Us, out):
 
         ident = const.tile([P, P], F32)
         make_identity(nc, ident[:])
+        ident_b = const.tile([P, P], BF16)
+        make_identity(nc, ident_b[:])
 
         one = const.tile([P, 1], F32)
         nc.vector.memset(one[:], 1.0)
@@ -180,6 +187,8 @@ def tile_moe_pa_t_kernel(tc, encodings, domain_encs, Us, out):
             b = take_bank()
             bank_of[("s", q)] = b
             enc_c, jj = enc_of_tile[b * TPB]
+            if plain(q):
+                return
             xf = xfp.tile([P, TPB * BPT, 2, WORDS], F32, name="xf")
             xf_of[q] = xf
             nc.scalar.copy(
@@ -194,14 +203,24 @@ def tile_moe_pa_t_kernel(tc, encodings, domain_encs, Us, out):
             acc_of[n] = acc
             for i2 in range(BPT):
                 for e in range(2):
-                    nc.tensor.matmul(
-                        out=acc[:, i2, e, :],
-                        lhsT=xf_of[q][:, j2 * BPT + i2, e, :],
-                        rhs=ident[:],
-                        is_transpose=True,
-                        start=True,
-                        stop=False,
-                    )
+                    if plain(q):
+                        enc_c, jj = enc_of_tile[bank_of[("s", q)] * TPB + j2]
+                        nc.tensor.matmul(
+                            out=acc[:, i2, e, :],
+                            lhsT=enc_c[:, jj * BPT + i2, e:HALF:2],
+                            rhs=ident_b[:],
+                            start=True,
+                            stop=False,
+                        )
+                    else:
+                        nc.tensor.matmul(
+                            out=acc[:, i2, e, :],
+                            lhsT=xf_of[q][:, j2 * BPT + i2, e, :],
+                            rhs=ident[:],
+                            is_transpose=True,
+                            start=True,
+                            stop=False,
+                        )
                     nc.tensor.matmul(
                         out=acc[:, i2, e, :],
                         lhsT=neg_dom[:, s, e, :],

@@ -29,15 +29,21 @@ NB = TILES // TPB
 GC = 36
 CV = COLS - GC
 NS = 12
+NP = 6
 NV = NB - NS
+LAST = NV - 1
 JOBS = NS * TPB * S
 T0 = 2
-T1 = NV - 2
+T1 = NV - 5
+QLAG = 2
 HEAD = 2
-NP = 6
-PROJ_BUFS = 3
+XT_BUFS = 3
+LEAD = 3
+PROJ_BUFS = 2
+ACC_BUFS = 3
 SMALL_CHUNKS = (2, 2, 4, 8)
 BIG = 16
+LATE = 8
 
 FLOPS = 2 * S * N_TOK * H * R
 
@@ -62,17 +68,17 @@ def tile_moe_pa_t_kernel(tc, encodings, domain_encs, Us, out):
         xfp = ctx.enter_context(tc.tile_pool(name="xfp", bufs=2))
         codep = ctx.enter_context(tc.tile_pool(name="codep", bufs=4))
         junkp = ctx.enter_context(tc.tile_pool(name="junkp", bufs=3))
-        xtp = ctx.enter_context(tc.psum_pool(name="xtp", bufs=3))
+        xtp = ctx.enter_context(tc.psum_pool(name="xtp", bufs=XT_BUFS))
         projp = ctx.enter_context(tc.psum_pool(name="projp", bufs=PROJ_BUFS))
-        accp = ctx.enter_context(tc.psum_pool(name="accp", bufs=2))
+        accp = ctx.enter_context(tc.psum_pool(name="accp", bufs=ACC_BUFS))
         ctx.enter_context(tc.manual_schedule())
 
-        dom_t = const.tile([P, S, PACK], BF16)
+        dom_t = const.tile([P, S, PACK], BF16, name="dom_t")
         nc.scalar.dma_start(
             out=dom_t[:].rearrange("p s (u e) -> p (s u) e", u=2),
             in_=domain_encs.rearrange("s (u p e) -> p (s u) e", u=2, p=P, e=2),
         )
-        raw_a = const.tile([P, S, PACK, R], BF16)
+        raw_a = const.tile([P, S, PACK, R], BF16, name="raw_a")
         nc.scalar.dma_start(
             out=raw_a[:].rearrange("p s (u e) r -> p (s u) (e r)", u=2),
             in_=Us.rearrange("s (u p e) r -> p (s u) (e r)", u=2, p=P, e=2),
@@ -98,7 +104,7 @@ def tile_moe_pa_t_kernel(tc, encodings, domain_encs, Us, out):
 
         for c in range(len(SMALL_CHUNKS)):
             load_chunk()
-        dom_rep = const.tile([P, S, HALF], BF16)
+        dom_rep = const.tile([P, S, HALF], BF16, name="dom_rep")
         for u in range(2):
             nc.sync.dma_start(
                 out=dom_rep[u:P:2, :, :], in_=domain_encs[:, u * HALF : (u + 1) * HALF].partition_broadcast(CT)
@@ -115,22 +121,23 @@ def tile_moe_pa_t_kernel(tc, encodings, domain_encs, Us, out):
                 load_chunk()
             return b
 
-        ident = const.tile([P, P], F32)
+        ident = const.tile([P, P], F32, name="ident")
         make_identity(nc, ident[:])
-        ident_b = const.tile([P, P], BF16)
+        ident_b = const.tile([P, P], BF16, name="ident_b")
         make_identity(nc, ident_b[:])
 
-        one = const.tile([P, 1], F32)
+        one = const.tile([P, 1], F32, name="one")
         nc.vector.memset(one[:], 1.0)
-        warm = const.tile([P, 1], F32)
+        warm = const.tile([P, 1], F32, name="warm")
         nc.scalar.activation(out=warm[:], in_=one[:], func=ACT.Sqrt)
 
-        grouped_a = const.tile([P, S, R, PACK], BF16, align_bytes=64)
-        ua_codes = const.tile([P, S * R], U32, align_bytes=64)
-        ua_scales = const.tile([P, S * R], U8, align_bytes=64)
-        neg_dom = const.tile([P, S, 2, WORDS], F32)
+        grouped_a = const.tile([P, S, R, PACK], BF16, name="grouped_a", align_bytes=64)
+        ua_codes = const.tile([P, S * R], U32, name="ua_codes", align_bytes=64)
+        ua_scales = const.tile([P, S * R], U8, name="ua_scales", align_bytes=64)
+        neg_dom = const.tile([P, S, 2, WORDS], F32, name="neg_dom")
 
-        d2 = const.tile([P, S, TILES], F32)
+        d2 = const.tile([P, S, TILES], F32, name="d2")
+        dist = const.tile([P, S, TILES], F32, name="dist")
 
         bank_of = {}
         xt_of = {}
@@ -162,13 +169,20 @@ def tile_moe_pa_t_kernel(tc, encodings, domain_encs, Us, out):
             xs_of[v] = xs
             nc.scalar.copy(out=xs[:], in_=xt_of[v][:, CV:COLS, :])
 
+        def part(v, c0, c1):
+            diff = diff_of[("v", v)]
+            if v == LAST:
+                j2 = c0 // P
+                return diff[:].rearrange("p (j s) c t -> p j s c t", j=TPB)[:, j2, :, c0 - j2 * P : c1 - j2 * P, :]
+            return diff[:].rearrange("p (s j) c t -> p s (j c) t", j=TPB)[:, :, c0:c1, :]
+
         def side_subtract(v):
-            diff = diffp.tile([P, S, COLS, PACK], BF16, name="diff", align_bytes=64)
+            diff = diffp.tile([P, S * TPB, P, PACK], BF16, name="diff", align_bytes=64)
             diff_of[("v", v)] = diff
             if v < HEAD:
                 return
             nc.gpsimd.tensor_tensor(
-                out=diff[:, :, CV:COLS, :],
+                out=part(v, CV, COLS),
                 in0=xs_of[v][:].bitcast(BF16).unsqueeze(1).to_broadcast([P, S, GC, PACK]),
                 in1=dom_t[:].unsqueeze(2).to_broadcast([P, S, GC, PACK]),
                 op=ALU.subtract,
@@ -176,12 +190,14 @@ def tile_moe_pa_t_kernel(tc, encodings, domain_encs, Us, out):
 
         def subtract(v):
             cv = COLS if v < HEAD else CV
-            nc.vector.tensor_tensor(
-                out=diff_of[("v", v)][:, :, 0:cv, :],
-                in0=xt_of[v][:, 0:cv, :].bitcast(BF16).unsqueeze(1).to_broadcast([P, S, cv, PACK]),
-                in1=dom_t[:].unsqueeze(2).to_broadcast([P, S, cv, PACK]),
-                op=ALU.subtract,
-            )
+            cuts = (0, P, cv) if v == LAST else (0, cv)
+            for c0, c1 in zip(cuts, cuts[1:]):
+                nc.vector.tensor_tensor(
+                    out=part(v, c0, c1),
+                    in0=xt_of[v][:, c0:c1, :].bitcast(BF16).unsqueeze(1).to_broadcast([P, S, c1 - c0, PACK]),
+                    in1=dom_t[:].unsqueeze(2).to_broadcast([P, S, c1 - c0, PACK]),
+                    op=ALU.subtract,
+                )
 
         def widen(q):
             b = take_bank()
@@ -234,10 +250,10 @@ def tile_moe_pa_t_kernel(tc, encodings, domain_encs, Us, out):
             q, k = divmod(n, TPB * S)
             j2, s = divmod(k, S)
             if k == 0:
-                diff_s = diffsp.tile([P, S, COLS, PACK], BF16, name="diff_s", align_bytes=64)
+                diff_s = diffsp.tile([P, S * TPB, P, PACK], BF16, name="diff_s", align_bytes=64)
                 diff_of[("s", q)] = diff_s
             nc.scalar.copy(
-                out=diff_of[("s", q)][:, s, j2 * P : (j2 + 1) * P, :]
+                out=diff_of[("s", q)][:, s * TPB + j2, :, :]
                 .rearrange("p c t -> p (c t)")
                 .rearrange("p (i x e) -> p i x e", i=BPT, e=2),
                 in_=acc_of[n][:].rearrange("p i e c -> p i c e"),
@@ -247,11 +263,15 @@ def tile_moe_pa_t_kernel(tc, encodings, domain_encs, Us, out):
             codes = codep.tile([P, S * COLS], U32, name="codes", align_bytes=64)
             scales = codep.tile([P, S * COLS], U8, name="scales", align_bytes=64)
             code_of[key] = (codes, scales)
-            nc.vector.quantize_mx(
-                out=codes[:].bitcast(FP8X4),
-                scales=scales[:],
-                in_=diff_of[key][:].rearrange("p s c t -> p (s c t)"),
-            )
+            flat = diff_of[key][:].rearrange("p k c t -> p (k c t)")
+            pieces = TPB if key == ("v", LAST) else 1
+            w = S * COLS // pieces
+            for h in range(pieces):
+                nc.vector.quantize_mx(
+                    out=codes[:, h * w : (h + 1) * w].bitcast(FP8X4),
+                    scales=scales[:, h * w : (h + 1) * w],
+                    in_=flat[:, h * w * PACK : (h + 1) * w * PACK],
+                )
 
         waiting = []
         squared = []
@@ -268,92 +288,114 @@ def tile_moe_pa_t_kernel(tc, encodings, domain_encs, Us, out):
                     accum_out=d2[:, s, tile_j : tile_j + 1],
                 )
 
-        def project(key):
+        def project(key, j2):
             codes, scales = code_of[key]
-            for j2 in range(TPB):
-                while len(waiting) - len(squared) >= PROJ_BUFS:
-                    squares()
-                proj = projp.tile([P, S * R], F32, name="proj")
-                for s in range(S):
-                    tok = slice(s * COLS + j2 * P, s * COLS + (j2 + 1) * P)
-                    rr = slice(s * R, (s + 1) * R)
-                    nc.tensor.matmul_mx(
-                        out=proj[:, rr],
-                        lhsT=codes[:, tok].bitcast(FP8X4),
-                        lhsT_scale=scales[:, tok],
-                        rhs=ua_codes[:, rr].bitcast(FP8X4),
-                        rhs_scale=ua_scales[:, rr],
-                        start=True,
-                        stop=True,
-                    )
-                waiting.append((proj, bank_of[key] * TPB + j2))
+            while len(waiting) - len(squared) >= PROJ_BUFS:
+                squares()
+            proj = projp.tile([P, S * R], F32, name="proj")
+            for s in range(S):
+                k = j2 * S + s if key == ("v", LAST) else s * TPB + j2
+                tok = slice(k * P, (k + 1) * P)
+                rr = slice(s * R, (s + 1) * R)
+                nc.tensor.matmul_mx(
+                    out=proj[:, rr],
+                    lhsT=codes[:, tok].bitcast(FP8X4),
+                    lhsT_scale=scales[:, tok],
+                    rhs=ua_codes[:, rr].bitcast(FP8X4),
+                    rhs_scale=ua_scales[:, rr],
+                    start=True,
+                    stop=True,
+                )
+            waiting.append((proj, bank_of[key] * TPB + j2))
 
         jobs_at = {}
         for n in range(JOBS):
             jobs_at[job_tick(n)] = jobs_at.get(job_tick(n), []) + [n]
         widen_at = dict((job_tick(q * TPB * S) - 1, q) for q in range(NS))
-        quant_at = dict((min(job_tick(q * TPB * S + TPB * S - 1) + 3, NV - 1), q) for q in range(NS))
+        quant_at = dict((job_tick(q * TPB * S + TPB * S - 1) + QLAG, q) for q in range(NS))
 
-        for v in range(3):
+        nc.scalar.copy(out=grouped_a[:], in_=raw_a[:].rearrange("p s t r -> p s r t"))
+        for v in range(LEAD):
             transposes(v)
+        for v in range(3):
             side_copy(v)
             side_subtract(v)
-        nc.scalar.copy(out=grouped_a[:], in_=raw_a[:].rearrange("p s t r -> p s r t"))
         subtract(0)
 
         for i in range(NV + 1):
-            if i + 3 < NV:
-                transposes(i + 3)
+            if i + LEAD < NV:
+                transposes(i + LEAD)
+            if LEAD > 3 and i + 3 < NV:
+                side_copy(i + 3)
             if i >= 1:
-                project(("v", i - 1))
-            if i - 1 in quant_at:
-                project(("s", quant_at[i - 1]))
+                project(("v", i - 1), 0)
+                project(("v", i - 1), 1)
+            if LEAD == 3 and i + 3 < NV:
+                side_copy(i + 3)
             if i == 1:
                 nc.scalar.mul(out=neg_dom[:], in_=dom_rep[:].rearrange("p s (w e) -> p s e w", e=2), mul=-1.0)
             for n in jobs_at.get(i - 1, []):
                 round_out(n)
             for n in jobs_at.get(i, []):
                 tensor_subtract(n)
-            if i + 3 < NV:
-                side_copy(i + 3)
+            if i - 1 in quant_at:
+                project(("s", quant_at[i - 1]), 0)
+                project(("s", quant_at[i - 1]), 1)
             if i in widen_at:
                 widen(widen_at[i])
             if i + 1 < NV:
                 subtract(i + 1)
+            if i in quant_at:
+                quantise(("s", quant_at[i]))
+            if i < NV:
+                quantise(("v", i))
             if i == 0:
                 nc.vector.quantize_mx(
                     out=ua_codes[:].bitcast(FP8X4),
                     scales=ua_scales[:],
                     in_=grouped_a[:].rearrange("p s r t -> p (s r t)"),
                 )
-            if i in quant_at:
-                quantise(("s", quant_at[i]))
-            if i < NV:
-                quantise(("v", i))
             if i + 3 < NV:
                 side_subtract(i + 3)
+            if i == NV - 2:
+                nc.scalar.activation(out=dist[:, :, 0 : TILES - LATE], in_=d2[:, :, 0 : TILES - LATE], func=ACT.Sqrt)
         while len(squared) < len(waiting):
             squares()
 
-        d2t = projp.tile([P, S * R], F32, name="proj")
+        nc.scalar.activation(
+            out=dist[:, :, TILES - LATE : TILES], in_=d2[:, :, TILES - LATE : TILES], func=ACT.Sqrt
+        )
+        dist_t = accp.tile([P, S, P], F32, name="acc")
         for s in range(S):
-            nc.tensor.transpose(d2t[:, s * P : (s + 1) * P], d2[:, s, :], ident[:])
-        dist = const.tile([P, S, P], F32)
-        nc.scalar.activation(out=dist[:].rearrange("j s p -> j (s p)"), in_=d2t[:], func=ACT.Sqrt)
-        low = const.tile([P, P], F32)
-        nc.vector.tensor_reduce(out=low[:], in_=dist[:].rearrange("j s p -> j p s"), axis=AX.X, op=ALU.min)
-        above = const.tile([P, S, P], F32)
-        nc.vector.tensor_tensor(
-            out=above[:], in0=dist[:], in1=low[:].unsqueeze(1).to_broadcast([P, S, P]), op=ALU.subtract
-        )
-        ex = const.tile([P, S, P], F32)
-        nc.scalar.activation(out=ex[:], in_=above[:], func=ACT.Exp, scale=-1.0)
-        total = const.tile([P, P], F32)
-        nc.vector.tensor_reduce(out=total[:], in_=ex[:].rearrange("j s p -> j p s"), axis=AX.X, op=ALU.add)
-        inv = const.tile([P, P], F32)
-        nc.vector.reciprocal(out=inv[:], in_=total[:])
-        res = const.tile([P, S, P], F32)
-        nc.vector.tensor_tensor(
-            out=res[:], in0=ex[:], in1=inv[:].unsqueeze(1).to_broadcast([P, S, P]), op=ALU.mult
-        )
-        nc.sync.dma_start(out=out.rearrange("s (j p) -> j s p", p=P), in_=res[:])
+            nc.tensor.transpose(dist_t[:, s, :], dist[:, s, :], ident[:])
+        low = const.tile([P, P], F32, name="low")
+        above = const.tile([P, S, P], F32, name="above")
+        ex = const.tile([P, S, P], F32, name="ex")
+        total = const.tile([P, P], F32, name="total")
+        inv = const.tile([P, P], F32, name="inv")
+        res = const.tile([P, S, P], F32, name="res")
+        halves = (slice(0, P // 2), slice(P // 2, P))
+        out_view = out.rearrange("s (j p) -> j s p", p=P)
+        for h in halves:
+            nc.vector.tensor_reduce(out=low[:, h], in_=dist_t[:, :, h].rearrange("j s p -> j p s"), axis=AX.X, op=ALU.min)
+        for h in halves:
+            nc.vector.tensor_tensor(
+                out=above[:, :, h],
+                in0=dist_t[:, :, h],
+                in1=low[:, h].unsqueeze(1).to_broadcast([P, S, P // 2]),
+                op=ALU.subtract,
+            )
+        for h in halves:
+            nc.scalar.activation(out=ex[:, :, h], in_=above[:, :, h], func=ACT.Exp, scale=-1.0)
+        for h in halves:
+            nc.vector.tensor_reduce(out=total[:, h], in_=ex[:, :, h].rearrange("j s p -> j p s"), axis=AX.X, op=ALU.add)
+        for h in halves:
+            nc.vector.reciprocal(out=inv[:, h], in_=total[:, h])
+        for h in halves:
+            nc.vector.tensor_tensor(
+                out=res[:, :, h],
+                in0=ex[:, :, h],
+                in1=inv[:, h].unsqueeze(1).to_broadcast([P, S, P // 2]),
+                op=ALU.mult,
+            )
+        nc.sync.dma_start(out=out_view, in_=res[:])

@@ -34,16 +34,16 @@ NV = NB - NS
 LAST = NV - 1
 JOBS = NS * TPB * S
 T0 = 2
-T1 = NV - 5
+T1 = NV - 2
 QLAG = 2
 HEAD = 2
 XT_BUFS = 3
 LEAD = 3
-PROJ_BUFS = 2
-ACC_BUFS = 3
+PROJ_BUFS = 3
+ACC_BUFS = 2
 SMALL_CHUNKS = (2, 2, 4, 8)
 BIG = 16
-LATE = 8
+LATE = 16
 
 FLOPS = 2 * S * N_TOK * H * R
 
@@ -188,16 +188,16 @@ def tile_moe_pa_t_kernel(tc, encodings, domain_encs, Us, out):
                 op=ALU.subtract,
             )
 
-        def subtract(v):
+        def subtract(v, j2=None):
             cv = COLS if v < HEAD else CV
-            cuts = (0, P, cv) if v == LAST else (0, cv)
-            for c0, c1 in zip(cuts, cuts[1:]):
-                nc.vector.tensor_tensor(
-                    out=part(v, c0, c1),
-                    in0=xt_of[v][:, c0:c1, :].bitcast(BF16).unsqueeze(1).to_broadcast([P, S, c1 - c0, PACK]),
-                    in1=dom_t[:].unsqueeze(2).to_broadcast([P, S, c1 - c0, PACK]),
-                    op=ALU.subtract,
-                )
+            cuts = (0, cv) if j2 is None else ((0, P), (P, cv))[j2]
+            c0, c1 = cuts
+            nc.vector.tensor_tensor(
+                out=part(v, c0, c1),
+                in0=xt_of[v][:, c0:c1, :].bitcast(BF16).unsqueeze(1).to_broadcast([P, S, c1 - c0, PACK]),
+                in1=dom_t[:].unsqueeze(2).to_broadcast([P, S, c1 - c0, PACK]),
+                op=ALU.subtract,
+            )
 
         def widen(q):
             b = take_bank()
@@ -343,12 +343,16 @@ def tile_moe_pa_t_kernel(tc, encodings, domain_encs, Us, out):
                 project(("s", quant_at[i - 1]), 1)
             if i in widen_at:
                 widen(widen_at[i])
-            if i + 1 < NV:
+            if i + 1 < LAST:
                 subtract(i + 1)
+            elif i + 1 == LAST:
+                subtract(LAST, 0)
             if i in quant_at:
                 quantise(("s", quant_at[i]))
             if i < NV:
                 quantise(("v", i))
+            if i + 1 == LAST:
+                subtract(LAST, 1)
             if i == 0:
                 nc.vector.quantize_mx(
                     out=ua_codes[:].bitcast(FP8X4),
@@ -398,4 +402,4 @@ def tile_moe_pa_t_kernel(tc, encodings, domain_encs, Us, out):
                 in1=inv[:, h].unsqueeze(1).to_broadcast([P, S, P // 2]),
                 op=ALU.mult,
             )
-        nc.sync.dma_start(out=out_view, in_=res[:])
+            nc.sync.dma_start(out=out_view[:, :, h], in_=res[:, :, h])

@@ -37,9 +37,9 @@ T0 = 2
 T1 = NV - 2
 QLAG = 2
 HEAD = 2
-XT_BUFS = 3
-LEAD = 3
-PROJ_BUFS = 3
+XT_BUFS = 4
+LEAD = 4
+PROJ_BUFS = 2
 ACC_BUFS = 2
 SMALL_CHUNKS = (2, 2, 4, 8)
 BIG = 16
@@ -73,11 +73,9 @@ def tile_moe_pa_t_kernel(tc, encodings, domain_encs, Us, out):
         accp = ctx.enter_context(tc.psum_pool(name="accp", bufs=ACC_BUFS))
         ctx.enter_context(tc.manual_schedule())
 
-        dom_t = const.tile([P, S, PACK], BF16, name="dom_t")
-        nc.scalar.dma_start(
-            out=dom_t[:].rearrange("p s (u e) -> p (s u) e", u=2),
-            in_=domain_encs.rearrange("s (u p e) -> p (s u) e", u=2, p=P, e=2),
-        )
+        dom_rows = const.tile([P, HALF], BF16, name="dom_rows")
+        nc.vector.memset(dom_rows[:], 0.0)
+        nc.scalar.dma_start(out=dom_rows[0 : 2 * S, :], in_=domain_encs.rearrange("s (u w) -> (s u) w", u=2))
         raw_a = const.tile([P, S, PACK, R], BF16, name="raw_a")
         nc.scalar.dma_start(
             out=raw_a[:].rearrange("p s (u e) r -> p (s u) (e r)", u=2),
@@ -125,6 +123,12 @@ def tile_moe_pa_t_kernel(tc, encodings, domain_encs, Us, out):
         make_identity(nc, ident[:])
         ident_b = const.tile([P, P], BF16, name="ident_b")
         make_identity(nc, ident_b[:])
+
+        dom_words = const.tile([P, 2 * S], F32, name="dom_words")
+        dom_ps = accp.tile([P, S, P], F32, name="acc")
+        nc.tensor.transpose(dom_ps[:, 0, :], dom_rows[:].bitcast(F32), ident[:])
+        nc.vector.tensor_copy(out=dom_words[:], in_=dom_ps[:, 0, 0 : 2 * S])
+        dom_t = dom_words[:].bitcast(BF16).rearrange("p (k t) -> p k t", k=S)
 
         one = const.tile([P, 1], F32, name="one")
         nc.vector.memset(one[:], 1.0)
@@ -184,7 +188,7 @@ def tile_moe_pa_t_kernel(tc, encodings, domain_encs, Us, out):
             nc.gpsimd.tensor_tensor(
                 out=part(v, CV, COLS),
                 in0=xs_of[v][:].bitcast(BF16).unsqueeze(1).to_broadcast([P, S, GC, PACK]),
-                in1=dom_t[:].unsqueeze(2).to_broadcast([P, S, GC, PACK]),
+                in1=dom_t.unsqueeze(2).to_broadcast([P, S, GC, PACK]),
                 op=ALU.subtract,
             )
 
@@ -195,7 +199,7 @@ def tile_moe_pa_t_kernel(tc, encodings, domain_encs, Us, out):
             nc.vector.tensor_tensor(
                 out=part(v, c0, c1),
                 in0=xt_of[v][:, c0:c1, :].bitcast(BF16).unsqueeze(1).to_broadcast([P, S, c1 - c0, PACK]),
-                in1=dom_t[:].unsqueeze(2).to_broadcast([P, S, c1 - c0, PACK]),
+                in1=dom_t.unsqueeze(2).to_broadcast([P, S, c1 - c0, PACK]),
                 op=ALU.subtract,
             )
 

@@ -33,8 +33,8 @@ NP = 6
 NV = NB - NS
 LAST = NV - 1
 JOBS = NS * TPB * S
-T0 = 2
-T1 = NV - 2
+T0 = 1
+T1 = NV - 3
 QLAG = 2
 HEAD = 2
 XT_BUFS = 4
@@ -49,7 +49,7 @@ FLOPS = 2 * S * N_TOK * H * R
 
 
 def plain(q):
-    return (q * NP) // NS != ((q + 1) * NP) // NS
+    return (q * NP) % NS < NP
 
 
 def job_tick(n):
@@ -74,15 +74,15 @@ def tile_moe_pa_t_kernel(tc, encodings, domain_encs, Us, out):
         ctx.enter_context(tc.manual_schedule())
 
         dom_rows = const.tile([P, HALF], BF16, name="dom_rows")
-        nc.vector.memset(dom_rows[:], 0.0)
-        nc.scalar.dma_start(out=dom_rows[0 : 2 * S, :], in_=domain_encs.rearrange("s (u w) -> (s u) w", u=2))
+        nc.sync.dma_start(out=dom_rows[0 : 2 * S, :], in_=domain_encs.rearrange("s (u w) -> (s u) w", u=2))
+        enc_view = encodings.rearrange("(j c) (u w) -> (c u) j w", c=CT, u=2)
+        nc.sync.dma_start(out=dom_rows[2 * S : P, :], in_=enc_view[2 * S : P, 0, :])
         raw_a = const.tile([P, S, PACK, R], BF16, name="raw_a")
         nc.scalar.dma_start(
             out=raw_a[:].rearrange("p s (u e) r -> p (s u) (e r)", u=2),
             in_=Us.rearrange("s (u p e) r -> p (s u) (e r)", u=2, p=P, e=2),
         )
 
-        enc_view = encodings.rearrange("(j c) (u w) -> (c u) j w", c=CT, u=2)
         enc_of_tile = []
         chunk_starts = []
 
@@ -124,16 +124,16 @@ def tile_moe_pa_t_kernel(tc, encodings, domain_encs, Us, out):
         ident_b = const.tile([P, P], BF16, name="ident_b")
         make_identity(nc, ident_b[:])
 
+        one = const.tile([P, 1], F32, name="one")
+        nc.vector.memset(one[:], 1.0)
+        warm = const.tile([P, 1], F32, name="warm")
+        nc.scalar.activation(out=warm[:], in_=one[:], func=ACT.Sqrt)
+
         dom_words = const.tile([P, 2 * S], F32, name="dom_words")
         dom_ps = accp.tile([P, S, P], F32, name="acc")
         nc.tensor.transpose(dom_ps[:, 0, :], dom_rows[:].bitcast(F32), ident[:])
         nc.vector.tensor_copy(out=dom_words[:], in_=dom_ps[:, 0, 0 : 2 * S])
         dom_t = dom_words[:].bitcast(BF16).rearrange("p (k t) -> p k t", k=S)
-
-        one = const.tile([P, 1], F32, name="one")
-        nc.vector.memset(one[:], 1.0)
-        warm = const.tile([P, 1], F32, name="warm")
-        nc.scalar.activation(out=warm[:], in_=one[:], func=ACT.Sqrt)
 
         grouped_a = const.tile([P, S, R, PACK], BF16, name="grouped_a", align_bytes=64)
         ua_codes = const.tile([P, S * R], U32, name="ua_codes", align_bytes=64)
@@ -292,11 +292,32 @@ def tile_moe_pa_t_kernel(tc, encodings, domain_encs, Us, out):
                     accum_out=d2[:, s, tile_j : tile_j + 1],
                 )
 
+        def vector_squares():
+            proj, tile_j = waiting[len(squared)]
+            squared.append(tile_j)
+            same = const.tile([P, S * R], F32, name="same")
+            nc.vector.tensor_copy(out=same[:], in_=proj[:])
+            product = const.tile([P, S * R], F32, name="product")
+            for s in range(S):
+                rr = slice(s * R, (s + 1) * R)
+                nc.vector.scalar_tensor_tensor(
+                    out=product[:, rr],
+                    in0=proj[:, rr],
+                    scalar=1.0,
+                    in1=same[:, rr],
+                    op0=ALU.mult,
+                    op1=ALU.mult,
+                    accum_out=d2[:, s, tile_j : tile_j + 1],
+                )
+
         def project(key, j2):
             codes, scales = code_of[key]
-            while len(waiting) - len(squared) >= PROJ_BUFS:
+            while key != ("v", LAST) and len(waiting) - len(squared) >= PROJ_BUFS:
                 squares()
-            proj = projp.tile([P, S * R], F32, name="proj")
+            if key == ("v", LAST):
+                proj = xtp.tile([P, S * R], F32, name="xt")
+            else:
+                proj = projp.tile([P, S * R], F32, name="proj")
             for s in range(S):
                 k = j2 * S + s if key == ("v", LAST) else s * TPB + j2
                 tok = slice(k * P, (k + 1) * P)
@@ -331,18 +352,21 @@ def tile_moe_pa_t_kernel(tc, encodings, domain_encs, Us, out):
                 transposes(i + LEAD)
             if LEAD > 3 and i + 3 < NV:
                 side_copy(i + 3)
+            if i == NV and i - 1 in quant_at:
+                project(("s", quant_at[i - 1]), 0)
+                project(("s", quant_at[i - 1]), 1)
             if i >= 1:
                 project(("v", i - 1), 0)
                 project(("v", i - 1), 1)
             if LEAD == 3 and i + 3 < NV:
                 side_copy(i + 3)
-            if i == 1:
+            if i == T0 - 1:
                 nc.scalar.mul(out=neg_dom[:], in_=dom_rep[:].rearrange("p s (w e) -> p s e w", e=2), mul=-1.0)
             for n in jobs_at.get(i - 1, []):
                 round_out(n)
             for n in jobs_at.get(i, []):
                 tensor_subtract(n)
-            if i - 1 in quant_at:
+            if i < NV and i - 1 in quant_at:
                 project(("s", quant_at[i - 1]), 0)
                 project(("s", quant_at[i - 1]), 1)
             if i in widen_at:
@@ -367,8 +391,11 @@ def tile_moe_pa_t_kernel(tc, encodings, domain_encs, Us, out):
                 side_subtract(i + 3)
             if i == NV - 2:
                 nc.scalar.activation(out=dist[:, :, 0 : TILES - LATE], in_=d2[:, :, 0 : TILES - LATE], func=ACT.Sqrt)
-        while len(squared) < len(waiting):
-            squares()
+        for k in range(len(squared), len(waiting)):
+            if k == len(waiting) - 3:
+                vector_squares()
+            else:
+                squares()
 
         nc.scalar.activation(
             out=dist[:, :, TILES - LATE : TILES], in_=d2[:, :, TILES - LATE : TILES], func=ACT.Sqrt

@@ -43,7 +43,9 @@ PROJ_BUFS = 2
 ACC_BUFS = 2
 SMALL_CHUNKS = (2, 2, 4, 8)
 BIG = 16
-LATE = 16
+ENDING = (("v", NV - 2), ("v", LAST))
+EARLY = NV - 6
+LATE = 32
 
 FLOPS = 2 * S * N_TOK * H * R
 
@@ -77,12 +79,6 @@ def tile_moe_pa_t_kernel(tc, encodings, domain_encs, Us, out):
         nc.sync.dma_start(out=dom_rows[0 : 2 * S, :], in_=domain_encs.rearrange("s (u w) -> (s u) w", u=2))
         enc_view = encodings.rearrange("(j c) (u w) -> (c u) j w", c=CT, u=2)
         nc.sync.dma_start(out=dom_rows[2 * S : P, :], in_=enc_view[2 * S : P, 0, :])
-        raw_a = const.tile([P, S, PACK, R], BF16, name="raw_a")
-        nc.scalar.dma_start(
-            out=raw_a[:].rearrange("p s (u e) r -> p (s u) (e r)", u=2),
-            in_=Us.rearrange("s (u p e) r -> p (s u) (e r)", u=2, p=P, e=2),
-        )
-
         enc_of_tile = []
         chunk_starts = []
 
@@ -100,8 +96,15 @@ def tile_moe_pa_t_kernel(tc, encodings, domain_encs, Us, out):
             for jj in range(n):
                 enc_of_tile.append((enc_c, jj))
 
-        for c in range(len(SMALL_CHUNKS)):
-            load_chunk()
+        load_chunk()
+        raw_a = const.tile([P, S, PACK, R], BF16, name="raw_a")
+        nc.sync.dma_start(
+            out=raw_a[:].rearrange("p s (u e) r -> p (s u) (e r)", u=2),
+            in_=Us.rearrange("s (u p e) r -> p (s u) (e r)", u=2, p=P, e=2),
+        )
+        load_chunk()
+        load_chunk()
+        load_chunk()
         dom_rep = const.tile([P, S, HALF], BF16, name="dom_rep")
         for u in range(2):
             nc.sync.dma_start(
@@ -312,9 +315,10 @@ def tile_moe_pa_t_kernel(tc, encodings, domain_encs, Us, out):
 
         def project(key, j2):
             codes, scales = code_of[key]
-            while key != ("v", LAST) and len(waiting) - len(squared) >= PROJ_BUFS:
+            free = key in ENDING
+            while not free and len(waiting) - len(squared) >= PROJ_BUFS:
                 squares()
-            if key == ("v", LAST):
+            if free:
                 proj = xtp.tile([P, S * R], F32, name="xt")
             else:
                 proj = projp.tile([P, S * R], F32, name="proj")
@@ -352,7 +356,7 @@ def tile_moe_pa_t_kernel(tc, encodings, domain_encs, Us, out):
                 transposes(i + LEAD)
             if LEAD > 3 and i + 3 < NV:
                 side_copy(i + 3)
-            if i == NV and i - 1 in quant_at:
+            if i >= NV - 1 and i - 1 in quant_at:
                 project(("s", quant_at[i - 1]), 0)
                 project(("s", quant_at[i - 1]), 1)
             if i >= 1:
@@ -362,11 +366,14 @@ def tile_moe_pa_t_kernel(tc, encodings, domain_encs, Us, out):
                 side_copy(i + 3)
             if i == T0 - 1:
                 nc.scalar.mul(out=neg_dom[:], in_=dom_rep[:].rearrange("p s (w e) -> p s e w", e=2), mul=-1.0)
-            for n in jobs_at.get(i - 1, []):
+            for n in jobs_at.get(i - 1, [])[-ACC_BUFS:]:
                 round_out(n)
-            for n in jobs_at.get(i, []):
+            todo = jobs_at.get(i, [])
+            for k, n in enumerate(todo):
+                if k >= ACC_BUFS:
+                    round_out(todo[k - ACC_BUFS])
                 tensor_subtract(n)
-            if i < NV and i - 1 in quant_at:
+            if i < NV - 1 and i - 1 in quant_at:
                 project(("s", quant_at[i - 1]), 0)
                 project(("s", quant_at[i - 1]), 1)
             if i in widen_at:
@@ -389,7 +396,7 @@ def tile_moe_pa_t_kernel(tc, encodings, domain_encs, Us, out):
                 )
             if i + 3 < NV:
                 side_subtract(i + 3)
-            if i == NV - 2:
+            if i == EARLY:
                 nc.scalar.activation(out=dist[:, :, 0 : TILES - LATE], in_=d2[:, :, 0 : TILES - LATE], func=ACT.Sqrt)
         for k in range(len(squared), len(waiting)):
             if k == len(waiting) - 3:

from contextlib import ExitStack

import concourse.mybir as mybir
from concourse.masks import make_identity

F32 = mybir.dt.float32
BF16 = mybir.dt.bfloat16
U32 = mybir.dt.uint32
U8 = mybir.dt.uint8
FP8X4 = mybir.dt.float8_e4m3fn_x4
ALU = mybir.AluOpType
ACT = mybir.ActivationFunctionType
AX = mybir.AxisListType

P = 128
N_TOK = 16384
H = 512
S = 4
R = 128
PACK = 4
TILES = N_TOK // P
HALF = H // 2
WORDS = HALF // 2
CT = P // 2
BPT = P // CT
TPB = 2
COLS = TPB * P
NB = TILES // TPB
GC = 36
CV = COLS - GC
NS = 12
NP = 6
NV = NB - NS
LAST = NV - 1
JOBS = NS * TPB * S
T0 = 1
T1 = NV - 3
QLAG = 2
HEAD = 2
XT_BUFS = 4
LEAD = 4
PROJ_BUFS = 2
ACC_BUFS = 2
SMALL_CHUNKS = (2, 2, 4, 8)
BIG = 16
ENDING = (("v", NV - 2), ("v", LAST))
EARLY = NV - 6
LATE = 32

FLOPS = 2 * S * N_TOK * H * R


def plain(q):
    return (q * NP) % NS < NP


def job_tick(n):
    return T0 + (n * (T1 - T0)) // JOBS


def tile_moe_pa_t_kernel(tc, encodings, domain_encs, Us, out):
    nc = tc.nc
    with ExitStack() as ctx:
        const = ctx.enter_context(tc.tile_pool(name="const", bufs=1))
        encp = ctx.enter_context(tc.tile_pool(name="encp", bufs=1))
        bigp = ctx.enter_context(tc.tile_pool(name="bigp", bufs=4))
        diffp = ctx.enter_context(tc.tile_pool(name="diffp", bufs=3))
        diffsp = ctx.enter_context(tc.tile_pool(name="diffsp", bufs=3))
        xsp = ctx.enter_context(tc.tile_pool(name="xsp", bufs=4))
        xfp = ctx.enter_context(tc.tile_pool(name="xfp", bufs=2))
        codep = ctx.enter_context(tc.tile_pool(name="codep", bufs=4))
        junkp = ctx.enter_context(tc.tile_pool(name="junkp", bufs=3))
        xtp = ctx.enter_context(tc.psum_pool(name="xtp", bufs=XT_BUFS))
        projp = ctx.enter_context(tc.psum_pool(name="projp", bufs=PROJ_BUFS))
        accp = ctx.enter_context(tc.psum_pool(name="accp", bufs=ACC_BUFS))
        ctx.enter_context(tc.manual_schedule())

        dom_rows = const.tile([P, HALF], BF16, name="dom_rows")
        nc.sync.dma_start(out=dom_rows[0 : 2 * S, :], in_=domain_encs.rearrange("s (u w) -> (s u) w", u=2))
        enc_view = encodings.rearrange("(j c) (u w) -> (c u) j w", c=CT, u=2)
        nc.sync.dma_start(out=dom_rows[2 * S : P, :], in_=enc_view[2 * S : P, 0, :])
        enc_of_tile = []
        chunk_starts = []

        def load_chunk():
            j0 = len(enc_of_tile)
            c = len(chunk_starts)
            chunk_starts.append(j0)
            if c < len(SMALL_CHUNKS):
                n = SMALL_CHUNKS[c]
                enc_c = encp.tile([P, n * BPT, HALF], BF16, name="enc%d" % c)
            else:
                n = BIG
                enc_c = bigp.tile([P, n * BPT, HALF], BF16, name="encbig")
            nc.sync.dma_start(out=enc_c[:], in_=enc_view[:, j0 * BPT : (j0 + n) * BPT, :])
            for jj in range(n):
                enc_of_tile.append((enc_c, jj))

        load_chunk()
        raw_a = const.tile([P, S, PACK, R], BF16, name="raw_a")
        nc.sync.dma_start(
            out=raw_a[:].rearrange("p s (u e) r -> p (s u) (e r)", u=2),
            in_=Us.rearrange("s (u p e) r -> p (s u) (e r)", u=2, p=P, e=2),
        )
        load_chunk()
        load_chunk()
        load_chunk()
        dom_rep = const.tile([P, S, HALF], BF16, name="dom_rep")
        for u in range(2):
            nc.sync.dma_start(
                out=dom_rep[u:P:2, :, :], in_=domain_encs[:, u * HALF : (u + 1) * HALF].partition_broadcast(CT)
            )
        load_chunk()
        load_chunk()

        banks = []

        def take_bank():
            b = len(banks)
            banks.append(b)
            if b * TPB in chunk_starts[len(SMALL_CHUNKS) :] and len(enc_of_tile) < TILES:
                load_chunk()
            return b

        ident = const.tile([P, P], F32, name="ident")
        make_identity(nc, ident[:])
        ident_b = const.tile([P, P], BF16, name="ident_b")
        make_identity(nc, ident_b[:])

        one = const.tile([P, 1], F32, name="one")
        nc.vector.memset(one[:], 1.0)
        warm = const.tile([P, 1], F32, name="warm")
        nc.scalar.activation(out=warm[:], in_=one[:], func=ACT.Sqrt)

        dom_words = const.tile([P, 2 * S], F32, name="dom_words")
        dom_ps = accp.tile([P, S, P], F32, name="acc")
        nc.tensor.transpose(dom_ps[:, 0, :], dom_rows[:].bitcast(F32), ident[:])
        nc.vector.tensor_copy(out=dom_words[:], in_=dom_ps[:, 0, 0 : 2 * S])
        dom_t = dom_words[:].bitcast(BF16).rearrange("p (k t) -> p k t", k=S)

        grouped_a = const.tile([P, S, R, PACK], BF16, name="grouped_a", align_bytes=64)
        ua_codes = const.tile([P, S * R], U32, name="ua_codes", align_bytes=64)
        ua_scales = const.tile([P, S * R], U8, name="ua_scales", align_bytes=64)
        neg_dom = const.tile([P, S, 2, WORDS], F32, name="neg_dom")

        d2 = const.tile([P, S, TILES], F32, name="d2")
        dist = const.tile([P, S, TILES], F32, name="dist")

        bank_of = {}
        xt_of = {}
        xs_of = {}
        diff_of = {}
        code_of = {}
        xf_of = {}
        acc_of = {}

        def transposes(v):
            b = take_bank()
            bank_of[("v", v)] = b
            xt = xtp.tile([P, COLS, 2], F32, name="xt")
            xt_of[v] = xt
            for j2 in range(TPB):
                enc_c, jj = enc_of_tile[b * TPB + j2]
                for i2 in range(BPT):
                    c0 = j2 * P + i2 * CT
                    nc.tensor.transpose(
                        xt[:, c0 : c0 + CT, :].rearrange("p c u -> p (c u)"),
                        enc_c[:, jj * BPT + i2, :].bitcast(F32),
                        ident[:],
                    )

        def side_copy(v):
            if v < HEAD:
                return
            xs = xsp.tile([P, GC, 2], F32, name="xs")
            xs_of[v] = xs
            nc.scalar.copy(out=xs[:], in_=xt_of[v][:, CV:COLS, :])

        def part(v, c0, c1):
            diff = diff_of[("v", v)]
            if v == LAST:
                j2 = c0 // P
                return diff[:].rearrange("p (j s) c t -> p j s c t", j=TPB)[:, j2, :, c0 - j2 * P : c1 - j2 * P, :]
            return diff[:].rearrange("p (s j) c t -> p s (j c) t", j=TPB)[:, :, c0:c1, :]

        def side_subtract(v):
            diff = diffp.tile([P, S * TPB, P, PACK], BF16, name="diff", align_bytes=64)
            diff_of[("v", v)] = diff
            if v < HEAD:
                return
            nc.gpsimd.tensor_tensor(
                out=part(v, CV, COLS),
                in0=xs_of[v][:].bitcast(BF16).unsqueeze(1).to_broadcast([P, S, GC, PACK]),
                in1=dom_t.unsqueeze(2).to_broadcast([P, S, GC, PACK]),
                op=ALU.subtract,
            )

        def subtract(v, j2=None):
            cv = COLS if v < HEAD else CV
            cuts = (0, cv) if j2 is None else ((0, P), (P, cv))[j2]
            c0, c1 = cuts
            nc.vector.tensor_tensor(
                out=part(v, c0, c1),
                in0=xt_of[v][:, c0:c1, :].bitcast(BF16).unsqueeze(1).to_broadcast([P, S, c1 - c0, PACK]),
                in1=dom_t.unsqueeze(2).to_broadcast([P, S, c1 - c0, PACK]),
                op=ALU.subtract,
            )

        def widen(q):
            b = take_bank()
            bank_of[("s", q)] = b
            enc_c, jj = enc_of_tile[b * TPB]
            if plain(q):
                return
            xf = xfp.tile([P, TPB * BPT, 2, WORDS], F32, name="xf")
            xf_of[q] = xf
            nc.scalar.copy(
                out=xf[:],
                in_=enc_c[:, jj * BPT : (jj + TPB) * BPT, :].rearrange("p j (w e) -> p j e w", e=2),
            )

        def tensor_subtract(n):
            q, k = divmod(n, TPB * S)
            j2, s = divmod(k, S)
            acc = accp.tile([P, BPT, 2, P], F32, name="acc")
            acc_of[n] = acc
            for i2 in range(BPT):
                for e in range(2):
                    if plain(q):
                        enc_c, jj = enc_of_tile[bank_of[("s", q)] * TPB + j2]
                        nc.tensor.matmul(
                            out=acc[:, i2, e, :],
                            lhsT=enc_c[:, jj * BPT + i2, e:HALF:2],
                            rhs=ident_b[:],
                            start=True,
                            stop=False,
                        )
                    else:
                        nc.tensor.matmul(
                            out=acc[:, i2, e, :],
                            lhsT=xf_of[q][:, j2 * BPT + i2, e, :],
                            rhs=ident[:],
                            is_transpose=True,
                            start=True,
                            stop=False,
                        )
                    nc.tensor.matmul(
                        out=acc[:, i2, e, :],
                        lhsT=neg_dom[:, s, e, :],
                        rhs=ident[:],
                        is_transpose=True,
                        start=False,
                        stop=True,
                    )

        def round_out(n):
            q, k = divmod(n, TPB * S)
            j2, s = divmod(k, S)
            if k == 0:
                diff_s = diffsp.tile([P, S * TPB, P, PACK], BF16, name="diff_s", align_bytes=64)
                diff_of[("s", q)] = diff_s
            nc.scalar.copy(
                out=diff_of[("s", q)][:, s * TPB + j2, :, :]
                .rearrange("p c t -> p (c t)")
                .rearrange("p (i x e) -> p i x e", i=BPT, e=2),
                in_=acc_of[n][:].rearrange("p i e c -> p i c e"),
            )

        def quantise(key):
            codes = codep.tile([P, S * COLS], U32, name="codes", align_bytes=64)
            scales = codep.tile([P, S * COLS], U8, name="scales", align_bytes=64)
            code_of[key] = (codes, scales)
            flat = diff_of[key][:].rearrange("p k c t -> p (k c t)")
            pieces = TPB if key == ("v", LAST) else 1
            w = S * COLS // pieces
            for h in range(pieces):
                nc.vector.quantize_mx(
                    out=codes[:, h * w : (h + 1) * w].bitcast(FP8X4),
                    scales=scales[:, h * w : (h + 1) * w],
                    in_=flat[:, h * w * PACK : (h + 1) * w * PACK],
                )

        waiting = []
        squared = []

        def squares():
            proj, tile_j = waiting[len(squared)]
            squared.append(tile_j)
            junk = junkp.tile([P, S, R], BF16, name="junk")
            for s in range(S):
                nc.scalar.activation(
                    out=junk[:, s, :],
                    in_=proj[:, s * R : (s + 1) * R],
                    func=ACT.Square,
                    accum_out=d2[:, s, tile_j : tile_j + 1],
                )

        def vector_squares():
            proj, tile_j = waiting[len(squared)]
            squared.append(tile_j)
            same = const.tile([P, S * R], F32, name="same")
            nc.vector.tensor_copy(out=same[:], in_=proj[:])
            product = const.tile([P, S * R], F32, name="product")
            for s in range(S):
                rr = slice(s * R, (s + 1) * R)
                nc.vector.scalar_tensor_tensor(
                    out=product[:, rr],
                    in0=proj[:, rr],
                    scalar=1.0,
                    in1=same[:, rr],
                    op0=ALU.mult,
                    op1=ALU.mult,
                    accum_out=d2[:, s, tile_j : tile_j + 1],
                )

        def project(key, j2):
            codes, scales = code_of[key]
            free = key in ENDING
            while not free and len(waiting) - len(squared) >= PROJ_BUFS:
                squares()
            if free:
                proj = xtp.tile([P, S * R], F32, name="xt")
            else:
                proj = projp.tile([P, S * R], F32, name="proj")
            for s in range(S):
                k = j2 * S + s if key == ("v", LAST) else s * TPB + j2
                tok = slice(k * P, (k + 1) * P)
                rr = slice(s * R, (s + 1) * R)
                nc.tensor.matmul_mx(
                    out=proj[:, rr],
                    lhsT=codes[:, tok].bitcast(FP8X4),
                    lhsT_scale=scales[:, tok],
                    rhs=ua_codes[:, rr].bitcast(FP8X4),
                    rhs_scale=ua_scales[:, rr],
                    start=True,
                    stop=True,
                )
            waiting.append((proj, bank_of[key] * TPB + j2))

        jobs_at = {}
        for n in range(JOBS):
            jobs_at[job_tick(n)] = jobs_at.get(job_tick(n), []) + [n]
        widen_at = dict((job_tick(q * TPB * S) - 1, q) for q in range(NS))
        quant_at = dict((job_tick(q * TPB * S + TPB * S - 1) + QLAG, q) for q in range(NS))

        nc.scalar.copy(out=grouped_a[:], in_=raw_a[:].rearrange("p s t r -> p s r t"))
        for v in range(LEAD):
            transposes(v)
        for v in range(3):
            side_copy(v)
            side_subtract(v)
        subtract(0)

        for i in range(NV + 1):
            if i + LEAD < NV:
                transposes(i + LEAD)
            if LEAD > 3 and i + 3 < NV:
                side_copy(i + 3)
            if i >= NV - 1 and i - 1 in quant_at:
                project(("s", quant_at[i - 1]), 0)
                project(("s", quant_at[i - 1]), 1)
            if i >= 1:
                project(("v", i - 1), 0)
                project(("v", i - 1), 1)
            if LEAD == 3 and i + 3 < NV:
                side_copy(i + 3)
            if i == T0 - 1:
                nc.scalar.mul(out=neg_dom[:], in_=dom_rep[:].rearrange("p s (w e) -> p s e w", e=2), mul=-1.0)
            for n in jobs_at.get(i - 1, [])[-ACC_BUFS:]:
                round_out(n)
            todo = jobs_at.get(i, [])
            for k, n in enumerate(todo):
                if k >= ACC_BUFS:
                    round_out(todo[k - ACC_BUFS])
                tensor_subtract(n)
            if i < NV - 1 and i - 1 in quant_at:
                project(("s", quant_at[i - 1]), 0)
                project(("s", quant_at[i - 1]), 1)
            if i in widen_at:
                widen(widen_at[i])
            if i + 1 < LAST:
                subtract(i + 1)
            elif i + 1 == LAST:
                subtract(LAST, 0)
            if i in quant_at:
                quantise(("s", quant_at[i]))
            if i < NV:
                quantise(("v", i))
            if i + 1 == LAST:
                subtract(LAST, 1)
            if i == 0:
                nc.vector.quantize_mx(
                    out=ua_codes[:].bitcast(FP8X4),
                    scales=ua_scales[:],
                    in_=grouped_a[:].rearrange("p s r t -> p (s r t)"),
                )
            if i + 3 < NV:
                side_subtract(i + 3)
            if i == EARLY:
                nc.scalar.activation(out=dist[:, :, 0 : TILES - LATE], in_=d2[:, :, 0 : TILES - LATE], func=ACT.Sqrt)
        for k in range(len(squared), len(waiting)):
            if k == len(waiting) - 3:
                vector_squares()
            else:
                squares()

        nc.scalar.activation(
            out=dist[:, :, TILES - LATE : TILES], in_=d2[:, :, TILES - LATE : TILES], func=ACT.Sqrt
        )
        dist_t = accp.tile([P, S, P], F32, name="acc")
        for s in range(S):
            nc.tensor.transpose(dist_t[:, s, :], dist[:, s, :], ident[:])
        low = const.tile([P, P], F32, name="low")
        above = const.tile([P, S, P], F32, name="above")
        ex = const.tile([P, S, P], F32, name="ex")
        total = const.tile([P, P], F32, name="total")
        inv = const.tile([P, P], F32, name="inv")
        res = const.tile([P, S, P], F32, name="res")
        halves = (slice(0, P // 2), slice(P // 2, P))
        out_view = out.rearrange("s (j p) -> j s p", p=P)
        for h in halves:
            nc.vector.tensor_reduce(out=low[:, h], in_=dist_t[:, :, h].rearrange("j s p -> j p s"), axis=AX.X, op=ALU.min)
        for h in halves:
            nc.vector.tensor_tensor(
                out=above[:, :, h],
                in0=dist_t[:, :, h],
                in1=low[:, h].unsqueeze(1).to_broadcast([P, S, P // 2]),
                op=ALU.subtract,
            )
        for h in halves:
            nc.scalar.activation(out=ex[:, :, h], in_=above[:, :, h], func=ACT.Exp, scale=-1.0)
        for h in halves:
            nc.vector.tensor_reduce(out=total[:, h], in_=ex[:, :, h].rearrange("j s p -> j p s"), axis=AX.X, op=ALU.add)
        for h in halves:
            nc.vector.reciprocal(out=inv[:, h], in_=total[:, h])
        for h in halves:
            nc.vector.tensor_tensor(
                out=res[:, :, h],
                in0=ex[:, :, h],
                in1=inv[:, h].unsqueeze(1).to_broadcast([P, S, P // 2]),
                op=ALU.mult,
            )
            nc.sync.dma_start(out=out_view[:, :, h], in_=res[:, :, h])
